import numpy as np
import ml_dtypes


def mxq(x, axis, fmt="e4m3"):
    dtype, down = {"e4m3": (ml_dtypes.float8_e4m3fn, 7), "e5m2": (ml_dtypes.float8_e5m2, 14)}[fmt]
    v = np.moveaxis(np.asarray(x, np.float32).astype(ml_dtypes.bfloat16).astype(np.float64), axis, -1)
    blocks = v.reshape(v.shape[:-1] + (-1, 32))
    amax = np.abs(blocks).max(-1, keepdims=True)
    byte = np.maximum(np.where(amax > 0, np.frexp(amax)[1] - 1 + 127, 0) - down, 1)
    scale = np.exp2(byte - 127.0)
    codes = (blocks / scale).astype(np.float32).astype(dtype).astype(np.float64)
    return np.moveaxis((codes * scale).reshape(v.shape), -1, axis)


WIDE = False


def mx_kscale(k):
    if not WIDE:
        return np.ones(k)
    levels = np.array([10, -10, 5, -5, 0])
    a = np.random.permutation(np.resize(levels, k // 512 * 4)).reshape(k // 512, 4)
    idx = np.arange(k)
    return np.exp2(a[idx // 512, idx % 128 // 32])


BF16 = ml_dtypes.bfloat16


def bf(x):
    return np.asarray(x, np.float32).astype(BF16)


def f64(x):
    return np.asarray(x).astype(np.float64)


B, S, D_IN, D_OUT, R = 2, 512, 4096, 4096, 512


def setup_inputs():
    t = mx_kscale(R)
    sk = t[np.arange(D_IN) % R]
    so = t[np.arange(D_OUT) * R // D_OUT]
    m_v = sk[:, None] == t[None, :]
    m_u = so[:, None] == t[None, :]
    g = R / m_u.sum(1)
    return {"x": bf(np.random.standard_normal((B, S, D_IN))),
            "U_latent": bf(np.random.standard_normal((D_OUT, R)) * 0.05 * m_u),
            "V_latent": bf(np.random.standard_normal((D_IN, R)) * 0.05 * m_v),
            "s1": bf(np.random.uniform(1.0, 4.0, D_OUT) / np.sqrt(R) * g / so),
            "s2": bf(np.random.uniform(0.25, 1.0, D_IN) / np.sqrt(D_IN) * sk),
            "bias": bf(np.random.standard_normal(D_OUT) * 0.5)}


def reference(x, U_latent, V_latent, s1, s2, bias):
    u_sign = np.sign(f64(U_latent))
    v_sign = np.sign(f64(V_latent))
    a = f64(x) * f64(s2)
    h = mxq(a, 2, "e4m3") @ mxq(v_sign, 0, "e4m3")
    z = mxq(h, 2, "e4m3") @ mxq(u_sign, 1, "e4m3").T
    return z * f64(s1) + f64(bias)

@@ -1,0 +1,266 @@
+from contextlib import ExitStack
+
+import concourse.masks as masks
+import concourse.mybir as mybir
+
+F32 = mybir.dt.float32
+BF16 = mybir.dt.bfloat16
+U32 = mybir.dt.uint32
+U8 = mybir.dt.uint8
+FP8X4 = mybir.dt.float8_e4m3fn_x4
+SIGN = mybir.ActivationFunctionType.Sign
+MULT = mybir.AluOpType.mult
+ADD = mybir.AluOpType.add
+
+P = 128
+PACK = 4
+K_PASS = P * PACK
+BANK = 512
+
+TOKENS = 1024
+D_IN = 4096
+D_OUT = 4096
+RANK = 512
+
+PASSES = D_IN // K_PASS
+TOKEN_TILES = TOKENS // P
+OUT_TILES = D_OUT // P
+PAIR = 2 * P
+ROUNDS = TOKENS // PAIR
+HALF = BANK
+STORE_COLS = 512
+
+FLOPS = 2 * TOKENS * D_IN * RANK + 2 * TOKENS * RANK * D_OUT
+
+
+def tile_binaryfactoredlinear_pa_kernel(tc, x, U_latent, V_latent, s1, s2, bias, out):
+    nc = tc.nc
+    x_rows = x.flatten_outer_dims()
+    v_view = V_latent.rearrange("(g u p e) r -> p g u (e r)", g=PASSES, u=2, p=P, e=2)
+    u_view = U_latent.rearrange("(c p) r -> p c r", p=P)
+    out_view = out.flatten_outer_dims().rearrange("(n p) o -> p n o", p=P)
+
+    with ExitStack() as whole_kernel:
+        consts = whole_kernel.enter_context(tc.tile_pool(name="consts", bufs=1))
+        keep = whole_kernel.enter_context(tc.tile_pool(name="keep", bufs=1))
+
+        identity = consts.tile([P, P], F32)
+        masks.make_identity(nc, identity[:])
+
+        u_words = keep.tile([P, D_OUT], U32, align_bytes=64)
+        u_scales = keep.tile([P, D_OUT], U8, align_bytes=64)
+        h_words = keep.tile([P, TOKENS], U32, align_bytes=64)
+        h_scales = keep.tile([P, TOKENS], U8, align_bytes=64)
+        s2_words = consts.tile([P, 2 * PASSES], F32)
+        gain_cols = consts.tile([P, 2 * OUT_TILES], F32)
+
+        with ExitStack() as phase1:
+            raw = phase1.enter_context(tc.tile_pool(name="raw", bufs=4))
+            grouped = phase1.enter_context(tc.tile_pool(name="grouped", bufs=2))
+            first = phase1.enter_context(tc.tile_pool(name="first", bufs=1))
+            turned = phase1.enter_context(tc.psum_pool(name="turned", bufs=6))
+            sums = phase1.enter_context(tc.psum_pool(name="sums", bufs=2))
+
+            v_words = first.tile([P, PASSES, RANK], U32, align_bytes=64)
+            v_scales = first.tile([P, PASSES, RANK], U8, align_bytes=64)
+            a_words = first.tile([P, ROUNDS, PASSES, PAIR], U32, align_bytes=64)
+            a_scales = first.tile([P, ROUNDS, PASSES, PAIR], U8, align_bytes=64)
+
+            s2_rows = first.tile([P, PAIR], BF16)
+            nc.vector.memset(s2_rows[:].bitcast(F32), 0.0)
+            nc.sync.dma_start(out=s2_rows[0 : 2 * PASSES, :], in_=s2.rearrange("(a w) -> a w", w=PAIR))
+            s2_turned = turned.tile([P, 2, PAIR], F32, tag="turned")
+            nc.tensor.transpose(s2_turned[:, 0, 0:P], s2_rows[:].bitcast(F32), identity[:])
+            nc.vector.tensor_copy(out=s2_words[:], in_=s2_turned[:, 0, 0 : 2 * PASSES])
+            s2_values = s2_words[:].bitcast(BF16)
+
+            def quantise_v_pass(g):
+                v_raw = raw.tile([P, PACK, RANK], BF16, tag="v_raw")
+                nc.sync.dma_start(out=v_raw[:].rearrange("p (u e) r -> p u (e r)", u=2), in_=v_view[:, g])
+                v_grouped = grouped.tile([P, RANK, PACK], BF16, tag="v_grouped", align_bytes=64)
+                for u in range(2):
+                    cols = slice(u * PAIR, (u + 1) * PAIR)
+                    nc.scalar.activation(
+                        out=v_grouped[:, cols, :].rearrange("p (e q) j -> p e q j", e=2),
+                        in_=v_raw[:, :, cols].rearrange("p j (q e) -> p e q j", e=2),
+                        func=SIGN,
+                    )
+                nc.vector.quantize_mx(
+                    out=v_words[:, g, :].bitcast(FP8X4),
+                    scales=v_scales[:, g, :],
+                    in_=v_grouped[:].rearrange("p c j -> p (c j)"),
+                )
+
+            def quantise_u_chunk(chunk):
+                tiles = 1024 // P
+                u_raw = raw.tile([P, tiles, RANK], BF16, tag="u_raw", bufs=2)
+                nc.sync.dma_start(out=u_raw[:], in_=u_view[:, chunk * tiles : (chunk + 1) * tiles, :])
+                u_grouped = grouped.tile([P, 1024, PACK], BF16, tag="u_grouped", align_bytes=64)
+                for b in range(tiles // 2):
+                    u_turned = turned.tile([P, 2, PAIR], F32, tag="turned")
+                    for u in range(2):
+                        for j in range(2):
+                            nc.tensor.transpose(
+                                u_turned[:, u, j * P : (j + 1) * P],
+                                u_raw[:, 2 * b + j, :].bitcast(F32)[:, u * P : (u + 1) * P],
+                                identity[:],
+                            )
+                    nc.scalar.activation(
+                        out=u_grouped[:, b * PAIR : (b + 1) * PAIR, :].rearrange("p o (u e) -> p o u e", u=2),
+                        in_=u_turned[:].bitcast(BF16).rearrange("p u (o e) -> p o u e", e=2),
+                        func=SIGN,
+                    )
+                cols = slice(chunk * 1024, (chunk + 1) * 1024)
+                nc.vector.quantize_mx(
+                    out=u_words[:, cols].bitcast(FP8X4),
+                    scales=u_scales[:, cols],
+                    in_=u_grouped[:].rearrange("p o j -> p (o j)"),
+                )
+
+            def quantise_a_pair(pair):
+                x_raw = []
+                for i in range(2):
+                    x_tile = raw.tile([P, D_IN], BF16, tag="x_raw")
+                    tile_rows = slice((2 * pair + i) * P, (2 * pair + i + 1) * P)
+                    nc.sync.dma_start(out=x_tile[:], in_=x_rows[tile_rows, :])
+                    x_raw.append(x_tile)
+                per_call = 4
+                for first_g in range(0, PASSES, per_call):
+                    a_grouped = grouped.tile([P, per_call, PAIR, PACK], BF16, tag="a_grouped", align_bytes=64)
+                    for n in range(per_call):
+                        g = first_g + n
+                        x_turned = turned.tile([P, 2, PAIR], F32, tag="turned")
+                        for u in range(2):
+                            for i in range(2):
+                                nc.tensor.transpose(
+                                    x_turned[:, u, i * P : (i + 1) * P],
+                                    x_raw[i][:].bitcast(F32)[:, (2 * g + u) * P : (2 * g + u + 1) * P],
+                                    identity[:],
+                                )
+                        gains = s2_values[:, g * PACK : (g + 1) * PACK].rearrange("p (o u e) -> p o u e", o=1, u=2)
+                        nc.vector.tensor_tensor(
+                            out=a_grouped[:, n, :, :].rearrange("p t (u e) -> p t u e", u=2),
+                            in0=x_turned[:].bitcast(BF16).rearrange("p u (t e) -> p t u e", e=2),
+                            in1=gains.to_broadcast([P, PAIR, 2, 2]),
+                            op=MULT,
+                        )
+                    passes = slice(first_g, first_g + per_call)
+                    nc.vector.quantize_mx(
+                        out=a_words[:, pair, passes, :].rearrange("p g t -> p (g t)").bitcast(FP8X4),
+                        scales=a_scales[:, pair, passes, :].rearrange("p g t -> p (g t)"),
+                        in_=a_grouped[:].rearrange("p g t j -> p (g t j)"),
+                    )
+
+            def first_matmul(pair):
+                h_grouped = grouped.tile([P, PAIR, PACK], BF16, tag="h_grouped", align_bytes=64)
+                for i in range(2):
+                    tokens = slice(i * P, (i + 1) * P)
+                    h_sums = sums.tile([P, PACK, P], F32, tag="h_sums")
+                    for j in range(PACK):
+                        cols = slice(j * P, (j + 1) * P)
+                        for g in range(PASSES):
+                            nc.tensor.matmul_mx(
+                                out=h_sums[:, j, :],
+                                lhsT=v_words[:, g, cols].bitcast(FP8X4),
+                                lhsT_scale=v_scales[:, g, cols],
+                                rhs=a_words[:, pair, g, tokens].bitcast(FP8X4),
+                                rhs_scale=a_scales[:, pair, g, tokens],
+                                start=(g == 0),
+                                stop=(g == PASSES - 1),
+                            )
+                    nc.scalar.copy(out=h_grouped[:, tokens, :], in_=h_sums[:].rearrange("p j t -> p t j"))
+                cols = slice(pair * PAIR, (pair + 1) * PAIR)
+                nc.vector.quantize_mx(
+                    out=h_words[:, cols].bitcast(FP8X4),
+                    scales=h_scales[:, cols],
+                    in_=h_grouped[:].rearrange("p t j -> p (t j)"),
+                )
+
+            for rnd in range(ROUNDS):
+                if rnd < ROUNDS // 2:
+                    for g in range(rnd * PASSES // 2, (rnd + 1) * PASSES // 2):
+                        quantise_v_pass(g)
+                else:
+                    for chunk in range(2 * rnd - ROUNDS, 2 * rnd - ROUNDS + 2):
+                        quantise_u_chunk(chunk)
+                quantise_a_pair(rnd)
+                if rnd == ROUNDS // 2 - 1:
+                    for pair in range(rnd):
+                        first_matmul(pair)
+                if rnd >= ROUNDS // 2 - 1:
+                    first_matmul(rnd)
+
+            gain_rows_bf16 = first.tile([P, P], BF16)
+            nc.vector.memset(gain_rows_bf16[:].bitcast(F32), 0.0)
+            nc.sync.dma_start(out=gain_rows_bf16[0:OUT_TILES, :], in_=s1.rearrange("(c p) -> c p", p=P))
+            nc.sync.dma_start(out=gain_rows_bf16[OUT_TILES : 2 * OUT_TILES, :], in_=bias.rearrange("(c p) -> c p", p=P))
+            gain_rows = first.tile([P, P], F32)
+            nc.vector.tensor_copy(out=gain_rows[:], in_=gain_rows_bf16[:])
+            gain_turned = turned.tile([P, 2, PAIR], F32, tag="turned")
+            nc.tensor.transpose(gain_turned[:, 0, 0:P], gain_rows[:], identity[:])
+            nc.vector.tensor_copy(out=gain_cols[:], in_=gain_turned[:, 0, 0 : 2 * OUT_TILES])
+
+        with ExitStack() as phase2:
+            scaled = phase2.enter_context(tc.tile_pool(name="scaled", bufs=4, reuse_waits="tile"))
+            results = phase2.enter_context(tc.tile_pool(name="results", bufs=3, reuse_waits="tile"))
+            products = phase2.enter_context(tc.psum_pool(name="products", bufs=4, reuse_waits="tile"))
+            back = phase2.enter_context(tc.psum_pool(name="back", bufs=4, reuse_waits="tile"))
+
+            tiles_per_half = HALF // P
+            units_per_half = OUT_TILES // 2
+            units_per_store = STORE_COLS // PAIR
+            units = (TOKENS // HALF) * units_per_half
+
+            def second_matmul(unit):
+                half, m = divmod(unit, units_per_half)
+                z_scaled = []
+                for j in range(2):
+                    c = 2 * m + j
+                    z_sums = products.tile([P, HALF], F32, tag="z_sums")
+                    nc.tensor.matmul_mx(
+                        out=z_sums[:],
+                        lhsT=u_words[:, c * P : (c + 1) * P].bitcast(FP8X4),
+                        lhsT_scale=u_scales[:, c * P : (c + 1) * P],
+                        rhs=h_words[:, half * HALF : (half + 1) * HALF].bitcast(FP8X4),
+                        rhs_scale=h_scales[:, half * HALF : (half + 1) * HALF],
+                        start=True,
+                        stop=True,
+                    )
+                    z_tile = scaled.tile([P, HALF], F32, tag="z_tile")
+                    nc.vector.tensor_scalar(
+                        out=z_tile[:],
+                        in0=z_sums[:],
+                        scalar1=gain_cols[:, c : c + 1],
+                        scalar2=gain_cols[:, OUT_TILES + c : OUT_TILES + c + 1],
+                        op0=MULT,
+                        op1=ADD,
+                    )
+                    z_scaled.append(z_tile)
+                return z_scaled
+
+            def turn_back(unit, z_scaled, result):
+                first_col = (unit % units_per_store) * PAIR
+                for a in range(tiles_per_half // 2):
+                    z_back = back.tile([P, 2, PAIR], F32, tag="z_back")
+                    for i in range(2):
+                        tokens = slice((2 * a + i) * P, (2 * a + i + 1) * P)
+                        for j in range(2):
+                            nc.tensor.transpose(z_back[:, i, j * P : (j + 1) * P], z_scaled[j][:, tokens], identity[:])
+                    nc.scalar.copy(out=result[:, 2 * a : 2 * a + 2, first_col : first_col + PAIR], in_=z_back[:])
+
+            waiting = second_matmul(0)
+            result = None
+            for unit in range(units):
+                ready = waiting
+                if unit + 1 < units:
+                    waiting = second_matmul(unit + 1)
+                if unit % units_per_store == 0:
+                    result = results.tile([P, tiles_per_half, STORE_COLS], F32, tag="result")
+                turn_back(unit, ready, result)
+                if unit % units_per_store == units_per_store - 1:
+                    half, m = divmod(unit, units_per_half)
+                    last_col = (m + 1) * PAIR
+                    nc.sync.dma_start(
+                        out=out_view[:, half * tiles_per_half : (half + 1) * tiles_per_half, last_col - STORE_COLS : last_col],
+                        in_=result[:],
+                    )

@@ -24,11 +24,17 @@ RANK = 512
 
 PASSES = D_IN // K_PASS
 TOKEN_TILES = TOKENS // P
-OUT_TILES = D_OUT // P
+SLICES = TOKEN_TILES
+V_SLICES = SLICES // 2
+V_PER_SLICE = PASSES // V_SLICES
+U_CHUNK = D_OUT // (SLICES - V_SLICES)
 PAIR = 2 * P
-ROUNDS = TOKENS // PAIR
+
 HALF = BANK
-STORE_COLS = 512
+TILES_PER_HALF = HALF // P
+TURNED_COLS = D_OUT // 2
+TURNED_TILES = TURNED_COLS // P
+BLOCK = BANK
 
 FLOPS = 2 * TOKENS * D_IN * RANK + 2 * TOKENS * RANK * D_OUT
 
@@ -41,6 +47,7 @@ def tile_binaryfactoredlinear_pa_kernel(tc, x, U_latent, V_latent, s1, s2, bias,
     out_view = out.flatten_outer_dims().rearrange("(n p) o -> p n o", p=P)
 
     with ExitStack() as whole_kernel:
+        whole_kernel.enter_context(tc.manual_schedule())
         consts = whole_kernel.enter_context(tc.tile_pool(name="consts", bufs=1))
         keep = whole_kernel.enter_context(tc.tile_pool(name="keep", bufs=1))
 
@@ -51,178 +58,223 @@ def tile_binaryfactoredlinear_pa_kernel(tc, x, U_latent, V_latent, s1, s2, bias,
         u_scales = keep.tile([P, D_OUT], U8, align_bytes=64)
         h_words = keep.tile([P, TOKENS], U32, align_bytes=64)
         h_scales = keep.tile([P, TOKENS], U8, align_bytes=64)
-        s2_words = consts.tile([P, 2 * PASSES], F32)
-        gain_cols = consts.tile([P, 2 * OUT_TILES], F32)
+        gain_cols = consts.tile([P, 2 * TURNED_TILES], F32)
+        s1_spread = consts.tile([P, D_OUT - TURNED_COLS], BF16)
+        bias_spread = consts.tile([P, D_OUT - TURNED_COLS], BF16)
 
         with ExitStack() as phase1:
             raw = phase1.enter_context(tc.tile_pool(name="raw", bufs=4))
             grouped = phase1.enter_context(tc.tile_pool(name="grouped", bufs=2))
             first = phase1.enter_context(tc.tile_pool(name="first", bufs=1))
-            turned = phase1.enter_context(tc.psum_pool(name="turned", bufs=6))
+            turned = phase1.enter_context(tc.psum_pool(name="turned", bufs=3))
             sums = phase1.enter_context(tc.psum_pool(name="sums", bufs=2))
 
             v_words = first.tile([P, PASSES, RANK], U32, align_bytes=64)
             v_scales = first.tile([P, PASSES, RANK], U8, align_bytes=64)
-            a_words = first.tile([P, ROUNDS, PASSES, PAIR], U32, align_bytes=64)
-            a_scales = first.tile([P, ROUNDS, PASSES, PAIR], U8, align_bytes=64)
 
-            s2_rows = first.tile([P, PAIR], BF16)
-            nc.vector.memset(s2_rows[:].bitcast(F32), 0.0)
-            nc.sync.dma_start(out=s2_rows[0 : 2 * PASSES, :], in_=s2.rearrange("(a w) -> a w", w=PAIR))
-            s2_turned = turned.tile([P, 2, PAIR], F32, tag="turned")
-            nc.tensor.transpose(s2_turned[:, 0, 0:P], s2_rows[:].bitcast(F32), identity[:])
-            nc.vector.tensor_copy(out=s2_words[:], in_=s2_turned[:, 0, 0 : 2 * PASSES])
-            s2_values = s2_words[:].bitcast(BF16)
-
-            def quantise_v_pass(g):
-                v_raw = raw.tile([P, PACK, RANK], BF16, tag="v_raw")
+            def load_v(g):
+                v_raw = raw.tile([P, PACK, RANK], BF16, tag="v_raw", bufs=PASSES)
                 nc.sync.dma_start(out=v_raw[:].rearrange("p (u e) r -> p u (e r)", u=2), in_=v_view[:, g])
-                v_grouped = grouped.tile([P, RANK, PACK], BF16, tag="v_grouped", align_bytes=64)
+                return v_raw
+
+            def load_u(chunk):
+                tiles = U_CHUNK // P
+                u_raw = raw.tile([P, tiles, RANK], BF16, tag="u_raw")
+                nc.sync.dma_start(out=u_raw[:], in_=u_view[:, chunk * tiles : (chunk + 1) * tiles, :])
+                return u_raw
+
+            def load_x(i):
+                x_raw = raw.tile([P, D_IN], BF16, tag="x_raw")
+                nc.sync.dma_start(out=x_raw[:], in_=x_rows[i * P : (i + 1) * P, :])
+                return x_raw
+
+            def sign_v(v_raw):
+                v_grouped = grouped.tile([P, RANK, PACK], BF16, tag="v_grouped", bufs=3, align_bytes=64)
                 for u in range(2):
                     cols = slice(u * PAIR, (u + 1) * PAIR)
                     nc.scalar.activation(
-                        out=v_grouped[:, cols, :].rearrange("p (e q) j -> p e q j", e=2),
-                        in_=v_raw[:, :, cols].rearrange("p j (q e) -> p e q j", e=2),
+                        out=v_grouped[:, cols, :].rearrange("p (e q) j -> p q j e", e=2),
+                        in_=v_raw[:, :, cols].rearrange("p j (q e) -> p q j e", e=2),
                         func=SIGN,
                     )
+                return v_grouped
+
+            def pack_v(g, v_grouped):
                 nc.vector.quantize_mx(
                     out=v_words[:, g, :].bitcast(FP8X4),
                     scales=v_scales[:, g, :],
                     in_=v_grouped[:].rearrange("p c j -> p (c j)"),
                 )
 
-            def quantise_u_chunk(chunk):
-                tiles = 1024 // P
-                u_raw = raw.tile([P, tiles, RANK], BF16, tag="u_raw", bufs=2)
-                nc.sync.dma_start(out=u_raw[:], in_=u_view[:, chunk * tiles : (chunk + 1) * tiles, :])
-                u_grouped = grouped.tile([P, 1024, PACK], BF16, tag="u_grouped", align_bytes=64)
-                for b in range(tiles // 2):
-                    u_turned = turned.tile([P, 2, PAIR], F32, tag="turned")
-                    for u in range(2):
-                        for j in range(2):
-                            nc.tensor.transpose(
-                                u_turned[:, u, j * P : (j + 1) * P],
-                                u_raw[:, 2 * b + j, :].bitcast(F32)[:, u * P : (u + 1) * P],
-                                identity[:],
-                            )
-                    nc.scalar.activation(
-                        out=u_grouped[:, b * PAIR : (b + 1) * PAIR, :].rearrange("p o (u e) -> p o u e", u=2),
-                        in_=u_turned[:].bitcast(BF16).rearrange("p u (o e) -> p o u e", e=2),
-                        func=SIGN,
-                    )
-                cols = slice(chunk * 1024, (chunk + 1) * 1024)
+            def turn_and_sign_u(u_raw, b, u_grouped):
+                u_turned = turned.tile([P, 2, PAIR], F32, tag="u_turned")
+                for u in range(2):
+                    for j in range(2):
+                        nc.tensor.transpose(
+                            u_turned[:, u, j * P : (j + 1) * P],
+                            u_raw[:, 2 * b + j, :].bitcast(F32)[:, u * P : (u + 1) * P],
+                            identity[:],
+                        )
+                nc.scalar.activation(
+                    out=u_grouped[:, b * PAIR : (b + 1) * PAIR, :].rearrange("p o (u e) -> p o u e", u=2),
+                    in_=u_turned[:].bitcast(BF16).rearrange("p u (o e) -> p o u e", e=2),
+                    func=SIGN,
+                )
+
+            def pack_u(chunk, u_grouped):
+                cols = slice(chunk * U_CHUNK, (chunk + 1) * U_CHUNK)
                 nc.vector.quantize_mx(
                     out=u_words[:, cols].bitcast(FP8X4),
                     scales=u_scales[:, cols],
                     in_=u_grouped[:].rearrange("p o j -> p (o j)"),
                 )
 
-            def quantise_a_pair(pair):
-                x_raw = []
-                for i in range(2):
-                    x_tile = raw.tile([P, D_IN], BF16, tag="x_raw")
-                    tile_rows = slice((2 * pair + i) * P, (2 * pair + i + 1) * P)
-                    nc.sync.dma_start(out=x_tile[:], in_=x_rows[tile_rows, :])
-                    x_raw.append(x_tile)
-                per_call = 4
-                for first_g in range(0, PASSES, per_call):
-                    a_grouped = grouped.tile([P, per_call, PAIR, PACK], BF16, tag="a_grouped", align_bytes=64)
-                    for n in range(per_call):
-                        g = first_g + n
-                        x_turned = turned.tile([P, 2, PAIR], F32, tag="turned")
-                        for u in range(2):
-                            for i in range(2):
-                                nc.tensor.transpose(
-                                    x_turned[:, u, i * P : (i + 1) * P],
-                                    x_raw[i][:].bitcast(F32)[:, (2 * g + u) * P : (2 * g + u + 1) * P],
-                                    identity[:],
-                                )
-                        gains = s2_values[:, g * PACK : (g + 1) * PACK].rearrange("p (o u e) -> p o u e", o=1, u=2)
-                        nc.vector.tensor_tensor(
-                            out=a_grouped[:, n, :, :].rearrange("p t (u e) -> p t u e", u=2),
-                            in0=x_turned[:].bitcast(BF16).rearrange("p u (t e) -> p t u e", e=2),
-                            in1=gains.to_broadcast([P, PAIR, 2, 2]),
-                            op=MULT,
+            def turn_and_scale_x(x_raw, b, a_grouped):
+                x_turned = turned.tile([P, 2, 2, P], F32, tag="x_turned")
+                for u in range(2):
+                    for n in range(2):
+                        first_word = (2 * (2 * b + n) + u) * P
+                        nc.tensor.transpose(
+                            x_turned[:, u, n, :], x_raw[:].bitcast(F32)[:, first_word : first_word + P], identity[:]
                         )
-                    passes = slice(first_g, first_g + per_call)
-                    nc.vector.quantize_mx(
-                        out=a_words[:, pair, passes, :].rearrange("p g t -> p (g t)").bitcast(FP8X4),
-                        scales=a_scales[:, pair, passes, :].rearrange("p g t -> p (g t)"),
-                        in_=a_grouped[:].rearrange("p g t j -> p (g t j)"),
-                    )
+                gains = s2_values[:, 2 * b * PACK : (2 * b + 2) * PACK]
+                nc.vector.tensor_tensor(
+                    out=a_grouped[:, 2 * b : 2 * b + 2, :, :].rearrange("p g t (u e) -> p g t u e", u=2),
+                    in0=x_turned[:].bitcast(BF16).rearrange("p u g (t e) -> p g t u e", e=2),
+                    in1=gains.rearrange("p (g o u e) -> p g o u e", g=2, o=1, u=2).to_broadcast([P, 2, P, 2, 2]),
+                    op=MULT,
+                )
 
-            def first_matmul(pair):
-                h_grouped = grouped.tile([P, PAIR, PACK], BF16, tag="h_grouped", align_bytes=64)
-                for i in range(2):
-                    tokens = slice(i * P, (i + 1) * P)
-                    h_sums = sums.tile([P, PACK, P], F32, tag="h_sums")
-                    for j in range(PACK):
-                        cols = slice(j * P, (j + 1) * P)
-                        for g in range(PASSES):
-                            nc.tensor.matmul_mx(
-                                out=h_sums[:, j, :],
-                                lhsT=v_words[:, g, cols].bitcast(FP8X4),
-                                lhsT_scale=v_scales[:, g, cols],
-                                rhs=a_words[:, pair, g, tokens].bitcast(FP8X4),
-                                rhs_scale=a_scales[:, pair, g, tokens],
-                                start=(g == 0),
-                                stop=(g == PASSES - 1),
-                            )
-                    nc.scalar.copy(out=h_grouped[:, tokens, :], in_=h_sums[:].rearrange("p j t -> p t j"))
-                cols = slice(pair * PAIR, (pair + 1) * PAIR)
+            def pack_a(a_grouped):
+                a_words = first.tile([P, PASSES, P], U32, tag="a_words", bufs=5, align_bytes=64)
+                a_scales = first.tile([P, PASSES, P], U8, tag="a_scales", bufs=5, align_bytes=64)
                 nc.vector.quantize_mx(
-                    out=h_words[:, cols].bitcast(FP8X4),
-                    scales=h_scales[:, cols],
+                    out=a_words[:].rearrange("p g t -> p (g t)").bitcast(FP8X4),
+                    scales=a_scales[:].rearrange("p g t -> p (g t)"),
+                    in_=a_grouped[:].rearrange("p g t j -> p (g t j)"),
+                )
+                return a_words, a_scales
+
+            def first_matmul(i, a_words, a_scales):
+                h_sums = sums.tile([P, PACK, P], F32, tag="h_sums")
+                for j in range(PACK):
+                    cols = slice(j * P, (j + 1) * P)
+                    for g in range(PASSES):
+                        nc.tensor.matmul_mx(
+                            out=h_sums[:, j, :],
+                            lhsT=v_words[:, g, cols].bitcast(FP8X4),
+                            lhsT_scale=v_scales[:, g, cols],
+                            rhs=a_words[:, g, :].bitcast(FP8X4),
+                            rhs_scale=a_scales[:, g, :],
+                            start=(g == 0),
+                            stop=(g == PASSES - 1),
+                        )
+                h_grouped = grouped.tile([P, P, PACK], BF16, tag="h_grouped", align_bytes=64)
+                nc.scalar.copy(out=h_grouped[:], in_=h_sums[:].rearrange("p j t -> p t j"))
+                tokens = slice(i * P, (i + 1) * P)
+                nc.vector.quantize_mx(
+                    out=h_words[:, tokens].bitcast(FP8X4),
+                    scales=h_scales[:, tokens],
                     in_=h_grouped[:].rearrange("p t j -> p (t j)"),
                 )
 
-            for rnd in range(ROUNDS):
-                if rnd < ROUNDS // 2:
-                    for g in range(rnd * PASSES // 2, (rnd + 1) * PASSES // 2):
-                        quantise_v_pass(g)
-                else:
-                    for chunk in range(2 * rnd - ROUNDS, 2 * rnd - ROUNDS + 2):
-                        quantise_u_chunk(chunk)
-                quantise_a_pair(rnd)
-                if rnd == ROUNDS // 2 - 1:
-                    for pair in range(rnd):
-                        first_matmul(pair)
-                if rnd >= ROUNDS // 2 - 1:
-                    first_matmul(rnd)
-
+            s2_rows = first.tile([P, PAIR], BF16)
+            nc.vector.memset(s2_rows[:].bitcast(F32), 0.0)
+            nc.sync.dma_start(out=s2_rows[0 : 2 * PASSES, :], in_=s2.rearrange("(a w) -> a w", w=PAIR))
             gain_rows_bf16 = first.tile([P, P], BF16)
             nc.vector.memset(gain_rows_bf16[:].bitcast(F32), 0.0)
-            nc.sync.dma_start(out=gain_rows_bf16[0:OUT_TILES, :], in_=s1.rearrange("(c p) -> c p", p=P))
-            nc.sync.dma_start(out=gain_rows_bf16[OUT_TILES : 2 * OUT_TILES, :], in_=bias.rearrange("(c p) -> c p", p=P))
+            nc.sync.dma_start(
+                out=gain_rows_bf16[0:TURNED_TILES, :], in_=s1[0:TURNED_COLS].rearrange("(c p) -> c p", p=P)
+            )
+            nc.sync.dma_start(
+                out=gain_rows_bf16[TURNED_TILES : 2 * TURNED_TILES, :],
+                in_=bias[0:TURNED_COLS].rearrange("(c p) -> c p", p=P),
+            )
+
+            v_raws = []
+            x_raws = []
+            u_raws = []
+            for s in range(V_SLICES):
+                v_raws.append(load_v(V_PER_SLICE * s))
+                x_raws.append(load_x(s))
+                v_raws.append(load_v(V_PER_SLICE * s + 1))
+
+            s2_turned = turned.tile([P, 2, 2, P], F32, tag="x_turned")
+            nc.tensor.transpose(s2_turned[:, 0, 0, :], s2_rows[:].bitcast(F32), identity[:])
+            s2_words = first.tile([P, 2 * PASSES], F32)
+            nc.vector.tensor_copy(out=s2_words[:], in_=s2_turned[:, 0, 0, 0 : 2 * PASSES])
+            s2_values = s2_words[:].bitcast(BF16)
             gain_rows = first.tile([P, P], F32)
             nc.vector.tensor_copy(out=gain_rows[:], in_=gain_rows_bf16[:])
-            gain_turned = turned.tile([P, 2, PAIR], F32, tag="turned")
-            nc.tensor.transpose(gain_turned[:, 0, 0:P], gain_rows[:], identity[:])
-            nc.vector.tensor_copy(out=gain_cols[:], in_=gain_turned[:, 0, 0 : 2 * OUT_TILES])
+            gain_turned = turned.tile([P, 2, 2, P], F32, tag="x_turned")
+            nc.tensor.transpose(gain_turned[:, 0, 0, :], gain_rows[:], identity[:])
+            nc.vector.tensor_copy(out=gain_cols[:], in_=gain_turned[:, 0, 0, 0 : 2 * TURNED_TILES])
+
+            a_packed = []
+            banks = PASSES // 2
+
+            odd_v = None
+            for s in range(V_SLICES):
+                if s > 0:
+                    pack_v(V_PER_SLICE * s - 1, odd_v)
+                even_v = sign_v(v_raws[V_PER_SLICE * s])
+                odd_v = sign_v(v_raws[V_PER_SLICE * s + 1])
+                a_grouped = grouped.tile([P, PASSES, P, PACK], BF16, tag="a_grouped", align_bytes=64)
+                for b in range(banks):
+                    turn_and_scale_x(x_raws[s], b, a_grouped)
+                pack_v(V_PER_SLICE * s, even_v)
+                a_packed.append(pack_a(a_grouped))
+                u_raws.append(load_u(s))
+                x_raws.append(load_x(s + V_SLICES))
+            pack_v(PASSES - 1, odd_v)
+
+            nc.sync.dma_start(out=s1_spread[:], in_=s1[TURNED_COLS:D_OUT].partition_broadcast(P))
+            nc.sync.dma_start(out=bias_spread[:], in_=bias[TURNED_COLS:D_OUT].partition_broadcast(P))
+
+            for s in range(V_SLICES, SLICES):
+                chunk = s - V_SLICES
+                a_grouped = grouped.tile([P, PASSES, P, PACK], BF16, tag="a_grouped", align_bytes=64)
+                u_grouped = grouped.tile([P, U_CHUNK, PACK], BF16, tag="u_grouped", align_bytes=64)
+                for b in range(banks):
+                    turn_and_sign_u(u_raws[chunk], b, u_grouped)
+                    turn_and_scale_x(x_raws[s], b, a_grouped)
+                a_packed.append(pack_a(a_grouped))
+                pack_u(chunk, u_grouped)
+                for i in range(2 * chunk, 2 * chunk + 2):
+                    first_matmul(i, a_packed[i][0], a_packed[i][1])
 
         with ExitStack() as phase2:
             scaled = phase2.enter_context(tc.tile_pool(name="scaled", bufs=4, reuse_waits="tile"))
             results = phase2.enter_context(tc.tile_pool(name="results", bufs=3, reuse_waits="tile"))
-            products = phase2.enter_context(tc.psum_pool(name="products", bufs=4, reuse_waits="tile"))
+            products = phase2.enter_context(tc.psum_pool(name="products", bufs=2, reuse_waits="tile"))
             back = phase2.enter_context(tc.psum_pool(name="back", bufs=4, reuse_waits="tile"))
 
-            tiles_per_half = HALF // P
-            units_per_half = OUT_TILES // 2
-            units_per_store = STORE_COLS // PAIR
-            units = (TOKENS // HALF) * units_per_half
+            units_per_block = 2
+            blocks = TURNED_COLS // BLOCK
+            units = (TOKENS // HALF) * blocks * units_per_block
 
-            def second_matmul(unit):
-                half, m = divmod(unit, units_per_half)
-                z_scaled = []
+            def place(unit):
+                half, rest = divmod(unit, blocks * units_per_block)
+                block, part = divmod(rest, units_per_block)
+                return half, block, part
+
+            def store(result, half, first_col):
+                token_tiles = slice(half * TILES_PER_HALF, (half + 1) * TILES_PER_HALF)
+                nc.sync.dma_start(out=out_view[:, token_tiles, first_col : first_col + BLOCK], in_=result[:])
+
+            def start_turned(unit):
+                half, block, part = place(unit)
+                tokens = slice(half * HALF, (half + 1) * HALF)
+                z_tiles = []
                 for j in range(2):
-                    c = 2 * m + j
+                    c = (block * units_per_block + part) * 2 + j
                     z_sums = products.tile([P, HALF], F32, tag="z_sums")
                     nc.tensor.matmul_mx(
                         out=z_sums[:],
                         lhsT=u_words[:, c * P : (c + 1) * P].bitcast(FP8X4),
                         lhsT_scale=u_scales[:, c * P : (c + 1) * P],
-                        rhs=h_words[:, half * HALF : (half + 1) * HALF].bitcast(FP8X4),
-                        rhs_scale=h_scales[:, half * HALF : (half + 1) * HALF],
+                        rhs=h_words[:, tokens].bitcast(FP8X4),
+                        rhs_scale=h_scales[:, tokens],
                         start=True,
                         stop=True,
                     )
@@ -231,36 +283,62 @@ def tile_binaryfactoredlinear_pa_kernel(tc, x, U_latent, V_latent, s1, s2, bias,
                         out=z_tile[:],
                         in0=z_sums[:],
                         scalar1=gain_cols[:, c : c + 1],
-                        scalar2=gain_cols[:, OUT_TILES + c : OUT_TILES + c + 1],
+                        scalar2=gain_cols[:, TURNED_TILES + c : TURNED_TILES + c + 1],
                         op0=MULT,
                         op1=ADD,
                     )
-                    z_scaled.append(z_tile)
-                return z_scaled
+                    z_tiles.append(z_tile)
+                return z_tiles
 
-            def turn_back(unit, z_scaled, result):
-                first_col = (unit % units_per_store) * PAIR
-                for a in range(tiles_per_half // 2):
+            def finish_turned(unit, z_tiles, result):
+                first_col = place(unit)[2] * PAIR
+                for a in range(TILES_PER_HALF // 2):
                     z_back = back.tile([P, 2, PAIR], F32, tag="z_back")
                     for i in range(2):
                         tokens = slice((2 * a + i) * P, (2 * a + i + 1) * P)
                         for j in range(2):
-                            nc.tensor.transpose(z_back[:, i, j * P : (j + 1) * P], z_scaled[j][:, tokens], identity[:])
+                            nc.tensor.transpose(z_back[:, i, j * P : (j + 1) * P], z_tiles[j][:, tokens], identity[:])
                     nc.scalar.copy(out=result[:, 2 * a : 2 * a + 2, first_col : first_col + PAIR], in_=z_back[:])
 
-            waiting = second_matmul(0)
-            result = None
-            for unit in range(units):
+            def direct(unit, result):
+                half, block, part = place(unit)
+                cols = slice(block * BLOCK, (block + 1) * BLOCK)
+                u_cols = slice(TURNED_COLS + block * BLOCK, TURNED_COLS + (block + 1) * BLOCK)
+                for j in range(2):
+                    i = 2 * part + j
+                    tokens = slice((half * TILES_PER_HALF + i) * P, (half * TILES_PER_HALF + i + 1) * P)
+                    z_direct = products.tile([P, BLOCK], F32, tag="z_direct")
+                    nc.tensor.matmul_mx(
+                        out=z_direct[:],
+                        lhsT=h_words[:, tokens].bitcast(FP8X4),
+                        lhsT_scale=h_scales[:, tokens],
+                        rhs=u_words[:, u_cols].bitcast(FP8X4),
+                        rhs_scale=u_scales[:, u_cols],
+                        start=True,
+                        stop=True,
+                    )
+                    z_gained = scaled.tile([P, BLOCK], F32, tag="z_gained")
+                    nc.vector.tensor_tensor(out=z_gained[:], in0=z_direct[:], in1=s1_spread[:, cols], op=MULT)
+                    nc.gpsimd.tensor_tensor(out=result[:, i, :], in0=z_gained[:], in1=bias_spread[:, cols], op=ADD)
+
+            result_turned = None
+            result_direct = None
+            waiting = None
+            for unit in range(-1, units):
                 ready = waiting
                 if unit + 1 < units:
-                    waiting = second_matmul(unit + 1)
-                if unit % units_per_store == 0:
-                    result = results.tile([P, tiles_per_half, STORE_COLS], F32, tag="result")
-                turn_back(unit, ready, result)
-                if unit % units_per_store == units_per_store - 1:
-                    half, m = divmod(unit, units_per_half)
-                    last_col = (m + 1) * PAIR
-                    nc.sync.dma_start(
-                        out=out_view[:, half * tiles_per_half : (half + 1) * tiles_per_half, last_col - STORE_COLS : last_col],
-                        in_=result[:],
-                    )
+                    waiting = start_turned(unit + 1)
+                if unit >= 0:
+                    half, block, part = place(unit)
+                    if part == 0:
+                        result_turned = results.tile([P, TILES_PER_HALF, BLOCK], F32, tag="result_turned")
+                    finish_turned(unit, ready, result_turned)
+                    if part == units_per_block - 1:
+                        store(result_turned, half, block * BLOCK)
+                if unit + 1 < units:
+                    half, block, part = place(unit + 1)
+                    if part == 0:
+                        result_direct = results.tile([P, TILES_PER_HALF, BLOCK], F32, tag="result_direct")
+                    direct(unit + 1, result_direct)
+                    if part == units_per_block - 1:
+                        store(result_direct, half, TURNED_COLS + block * BLOCK)

@@ -9,6 +9,7 @@ U32 = mybir.dt.uint32
 U8 = mybir.dt.uint8
 FP8X4 = mybir.dt.float8_e4m3fn_x4
 SIGN = mybir.ActivationFunctionType.Sign
+IDENTITY = mybir.ActivationFunctionType.Identity
 MULT = mybir.AluOpType.mult
 ADD = mybir.AluOpType.add
 
@@ -24,17 +25,19 @@ RANK = 512
 
 PASSES = D_IN // K_PASS
 TOKEN_TILES = TOKENS // P
-SLICES = TOKEN_TILES
-V_SLICES = SLICES // 2
-V_PER_SLICE = PASSES // V_SLICES
-U_CHUNK = D_OUT // (SLICES - V_SLICES)
-PAIR = 2 * P
-
 HALF = BANK
 TILES_PER_HALF = HALF // P
-TURNED_COLS = D_OUT // 2
-TURNED_TILES = TURNED_COLS // P
+SLICES = 4
+V_PER_SLICE = PASSES // SLICES
+X_COLS = V_PER_SLICE * K_PASS
+U_CHUNK = D_OUT // SLICES
+PAIR = 2 * P
+
 BLOCK = BANK
+TURNED_BLOCKS = 5
+TURNED_COLS = TURNED_BLOCKS * BLOCK
+TURNED_TILES = TURNED_COLS // P
+DIRECT_BLOCKS = D_OUT // BLOCK - TURNED_BLOCKS
 
 FLOPS = 2 * TOKENS * D_IN * RANK + 2 * TOKENS * RANK * D_OUT
 
@@ -42,303 +45,361 @@ FLOPS = 2 * TOKENS * D_IN * RANK + 2 * TOKENS * RANK * D_OUT
 def tile_binaryfactoredlinear_pa_kernel(tc, x, U_latent, V_latent, s1, s2, bias, out):
     nc = tc.nc
     x_rows = x.flatten_outer_dims()
+    x_first = x_rows[0:HALF, :].rearrange("(n p) k -> p n k", p=P)
     v_view = V_latent.rearrange("(g u p e) r -> p g u (e r)", g=PASSES, u=2, p=P, e=2)
     u_view = U_latent.rearrange("(c p) r -> p c r", p=P)
     out_view = out.flatten_outer_dims().rearrange("(n p) o -> p n o", p=P)
 
-    with ExitStack() as whole_kernel:
-        whole_kernel.enter_context(tc.manual_schedule())
-        consts = whole_kernel.enter_context(tc.tile_pool(name="consts", bufs=1))
-        keep = whole_kernel.enter_context(tc.tile_pool(name="keep", bufs=1))
+    with ExitStack() as stack:
+        stack.enter_context(tc.manual_schedule())
+        consts = stack.enter_context(tc.tile_pool(name="consts", bufs=1))
+        pool = stack.enter_context(tc.tile_pool(name="pool", bufs=2))
+        psum = stack.enter_context(tc.psum_pool(name="psum", bufs=4))
 
         identity = consts.tile([P, P], F32)
         masks.make_identity(nc, identity[:])
 
-        u_words = keep.tile([P, D_OUT], U32, align_bytes=64)
-        u_scales = keep.tile([P, D_OUT], U8, align_bytes=64)
-        h_words = keep.tile([P, TOKENS], U32, align_bytes=64)
-        h_scales = keep.tile([P, TOKENS], U8, align_bytes=64)
+        v_words = consts.tile([P, PASSES, RANK], U32, align_bytes=64)
+        v_scales = consts.tile([P, PASSES, RANK], U8, align_bytes=64)
+        u_words = consts.tile([P, D_OUT], U32, align_bytes=64)
+        u_scales = consts.tile([P, D_OUT], U8, align_bytes=64)
+        h_words = consts.tile([P, TOKENS], U32, align_bytes=64)
+        h_scales = consts.tile([P, TOKENS], U8, align_bytes=64)
         gain_cols = consts.tile([P, 2 * TURNED_TILES], F32)
         s1_spread = consts.tile([P, D_OUT - TURNED_COLS], BF16)
         bias_spread = consts.tile([P, D_OUT - TURNED_COLS], BF16)
 
-        with ExitStack() as phase1:
-            raw = phase1.enter_context(tc.tile_pool(name="raw", bufs=4))
-            grouped = phase1.enter_context(tc.tile_pool(name="grouped", bufs=2))
-            first = phase1.enter_context(tc.tile_pool(name="first", bufs=1))
-            turned = phase1.enter_context(tc.psum_pool(name="turned", bufs=3))
-            sums = phase1.enter_context(tc.psum_pool(name="sums", bufs=2))
+        def big_tile(shape, dtype):
+            tile = pool.tile(shape, dtype, tag="big", bufs=10, name="big")
+            return tile
 
-            v_words = first.tile([P, PASSES, RANK], U32, align_bytes=64)
-            v_scales = first.tile([P, PASSES, RANK], U8, align_bytes=64)
+        def load_v(v_raw, g):
+            nc.sync.dma_start(
+                out=v_raw[:, g % V_PER_SLICE].rearrange("p (u e) r -> p u (e r)", u=2), in_=v_view[:, g]
+            )
 
-            def load_v(g):
-                v_raw = raw.tile([P, PACK, RANK], BF16, tag="v_raw", bufs=PASSES)
-                nc.sync.dma_start(out=v_raw[:].rearrange("p (u e) r -> p u (e r)", u=2), in_=v_view[:, g])
-                return v_raw
+        def load_u(chunk):
+            tiles = U_CHUNK // P
+            u_raw = big_tile([P, tiles, RANK], BF16)
+            nc.sync.dma_start(out=u_raw[:], in_=u_view[:, chunk * tiles : (chunk + 1) * tiles, :])
+            return u_raw
 
-            def load_u(chunk):
-                tiles = U_CHUNK // P
-                u_raw = raw.tile([P, tiles, RANK], BF16, tag="u_raw")
-                nc.sync.dma_start(out=u_raw[:], in_=u_view[:, chunk * tiles : (chunk + 1) * tiles, :])
-                return u_raw
+        def load_x(i):
+            x_raw = big_tile([P, D_IN], BF16)
+            nc.sync.dma_start(out=x_raw[:], in_=x_rows[i * P : (i + 1) * P, :])
+            return x_raw
 
-            def load_x(i):
-                x_raw = raw.tile([P, D_IN], BF16, tag="x_raw")
-                nc.sync.dma_start(out=x_raw[:], in_=x_rows[i * P : (i + 1) * P, :])
-                return x_raw
-
-            def sign_v(v_raw):
-                v_grouped = grouped.tile([P, RANK, PACK], BF16, tag="v_grouped", bufs=3, align_bytes=64)
-                for u in range(2):
-                    cols = slice(u * PAIR, (u + 1) * PAIR)
-                    nc.scalar.activation(
-                        out=v_grouped[:, cols, :].rearrange("p (e q) j -> p q j e", e=2),
-                        in_=v_raw[:, :, cols].rearrange("p j (q e) -> p q j e", e=2),
-                        func=SIGN,
-                    )
-                return v_grouped
-
-            def pack_v(g, v_grouped):
-                nc.vector.quantize_mx(
-                    out=v_words[:, g, :].bitcast(FP8X4),
-                    scales=v_scales[:, g, :],
-                    in_=v_grouped[:].rearrange("p c j -> p (c j)"),
-                )
-
-            def turn_and_sign_u(u_raw, b, u_grouped):
-                u_turned = turned.tile([P, 2, PAIR], F32, tag="u_turned")
-                for u in range(2):
-                    for j in range(2):
-                        nc.tensor.transpose(
-                            u_turned[:, u, j * P : (j + 1) * P],
-                            u_raw[:, 2 * b + j, :].bitcast(F32)[:, u * P : (u + 1) * P],
-                            identity[:],
-                        )
+        def sign_v(v_raw, g):
+            v_grouped = pool.tile([P, RANK, PACK], BF16, tag="v_grouped", bufs=3, align_bytes=64)
+            for u in range(2):
+                cols = slice(u * PAIR, (u + 1) * PAIR)
                 nc.scalar.activation(
-                    out=u_grouped[:, b * PAIR : (b + 1) * PAIR, :].rearrange("p o (u e) -> p o u e", u=2),
-                    in_=u_turned[:].bitcast(BF16).rearrange("p u (o e) -> p o u e", e=2),
+                    out=v_grouped[:, cols, :].rearrange("p (e q) j -> p q j e", e=2),
+                    in_=v_raw[:, g % V_PER_SLICE, :, cols].rearrange("p j (q e) -> p q j e", e=2),
                     func=SIGN,
                 )
+            return v_grouped
 
-            def pack_u(chunk, u_grouped):
-                cols = slice(chunk * U_CHUNK, (chunk + 1) * U_CHUNK)
-                nc.vector.quantize_mx(
-                    out=u_words[:, cols].bitcast(FP8X4),
-                    scales=u_scales[:, cols],
-                    in_=u_grouped[:].rearrange("p o j -> p (o j)"),
-                )
+        def pack_v(g, v_grouped):
+            nc.vector.quantize_mx(
+                out=v_words[:, g, :].bitcast(FP8X4),
+                scales=v_scales[:, g, :],
+                in_=v_grouped[:].rearrange("p c j -> p (c j)"),
+            )
 
-            def turn_and_scale_x(x_raw, b, a_grouped):
-                x_turned = turned.tile([P, 2, 2, P], F32, tag="x_turned")
-                for u in range(2):
-                    for n in range(2):
-                        first_word = (2 * (2 * b + n) + u) * P
-                        nc.tensor.transpose(
-                            x_turned[:, u, n, :], x_raw[:].bitcast(F32)[:, first_word : first_word + P], identity[:]
-                        )
-                gains = s2_values[:, 2 * b * PACK : (2 * b + 2) * PACK]
-                nc.vector.tensor_tensor(
-                    out=a_grouped[:, 2 * b : 2 * b + 2, :, :].rearrange("p g t (u e) -> p g t u e", u=2),
-                    in0=x_turned[:].bitcast(BF16).rearrange("p u g (t e) -> p g t u e", e=2),
-                    in1=gains.rearrange("p (g o u e) -> p g o u e", g=2, o=1, u=2).to_broadcast([P, 2, P, 2, 2]),
-                    op=MULT,
-                )
+        def turn_and_sign_u(u_raw, b, u_grouped):
+            u_turned = psum.tile([P, 2, PAIR], F32, tag="turned")
+            for u in range(2):
+                for j in range(2):
+                    nc.tensor.transpose(
+                        u_turned[:, u, j * P : (j + 1) * P],
+                        u_raw[:, 2 * b + j, :].bitcast(F32)[:, u * P : (u + 1) * P],
+                        identity[:],
+                    )
+            nc.scalar.activation(
+                out=u_grouped[:, b * PAIR : (b + 1) * PAIR, :].rearrange("p o (u e) -> p o u e", u=2),
+                in_=u_turned[:].bitcast(BF16).rearrange("p u (o e) -> p o u e", e=2),
+                func=SIGN,
+            )
 
-            def pack_a(a_grouped):
-                a_words = first.tile([P, PASSES, P], U32, tag="a_words", bufs=5, align_bytes=64)
-                a_scales = first.tile([P, PASSES, P], U8, tag="a_scales", bufs=5, align_bytes=64)
-                nc.vector.quantize_mx(
-                    out=a_words[:].rearrange("p g t -> p (g t)").bitcast(FP8X4),
-                    scales=a_scales[:].rearrange("p g t -> p (g t)"),
-                    in_=a_grouped[:].rearrange("p g t j -> p (g t j)"),
-                )
-                return a_words, a_scales
+        def pack_u(chunk, u_grouped):
+            cols = slice(chunk * U_CHUNK, (chunk + 1) * U_CHUNK)
+            nc.vector.quantize_mx(
+                out=u_words[:, cols].bitcast(FP8X4),
+                scales=u_scales[:, cols],
+                in_=u_grouped[:].rearrange("p o j -> p (o j)"),
+            )
 
-            def first_matmul(i, a_words, a_scales):
-                h_sums = sums.tile([P, PACK, P], F32, tag="h_sums")
+        def turn_and_scale_x(x_piece, g, a_piece):
+            x_turned = psum.tile([P, 2, 2, P], F32, tag="turned")
+            for u in range(2):
+                for n in range(2):
+                    first_word = (2 * n + u) * P
+                    nc.tensor.transpose(
+                        x_turned[:, u, n, :], x_piece.bitcast(F32)[:, first_word : first_word + P], identity[:]
+                    )
+            gains = s2_values[:, g * PACK : (g + 2) * PACK]
+            nc.vector.tensor_tensor(
+                out=a_piece.rearrange("p g t (u e) -> p g t u e", u=2),
+                in0=x_turned[:].bitcast(BF16).rearrange("p u g (t e) -> p g t u e", e=2),
+                in1=gains.rearrange("p (g o u e) -> p g o u e", g=2, o=1, u=2).to_broadcast([P, 2, P, 2, 2]),
+                op=MULT,
+            )
+
+        def pack_a(a_grouped, passes, tokens):
+            a_words = pool.tile([P, passes, tokens], U32, tag="a_words", bufs=3, align_bytes=64)
+            a_scales = pool.tile([P, passes, tokens], U8, tag="a_scales", bufs=3, align_bytes=64)
+            nc.vector.quantize_mx(
+                out=a_words[:].rearrange("p g t -> p (g t)").bitcast(FP8X4),
+                scales=a_scales[:].rearrange("p g t -> p (g t)"),
+                in_=a_grouped[:].rearrange("p g t j -> p (g t j)"),
+            )
+            return a_words, a_scales
+
+        def first_matmul_slice(s, a_packed, h_open):
+            a_words, a_scales = a_packed
+            for n in range(V_PER_SLICE):
+                g = V_PER_SLICE * s + n
                 for j in range(PACK):
                     cols = slice(j * P, (j + 1) * P)
-                    for g in range(PASSES):
-                        nc.tensor.matmul_mx(
-                            out=h_sums[:, j, :],
-                            lhsT=v_words[:, g, cols].bitcast(FP8X4),
-                            lhsT_scale=v_scales[:, g, cols],
-                            rhs=a_words[:, g, :].bitcast(FP8X4),
-                            rhs_scale=a_scales[:, g, :],
-                            start=(g == 0),
-                            stop=(g == PASSES - 1),
-                        )
-                h_grouped = grouped.tile([P, P, PACK], BF16, tag="h_grouped", align_bytes=64)
-                nc.scalar.copy(out=h_grouped[:], in_=h_sums[:].rearrange("p j t -> p t j"))
-                tokens = slice(i * P, (i + 1) * P)
-                nc.vector.quantize_mx(
-                    out=h_words[:, tokens].bitcast(FP8X4),
-                    scales=h_scales[:, tokens],
-                    in_=h_grouped[:].rearrange("p t j -> p (t j)"),
+                    nc.tensor.matmul_mx(
+                        out=h_open[j][:],
+                        lhsT=v_words[:, g, cols].bitcast(FP8X4),
+                        lhsT_scale=v_scales[:, g, cols],
+                        rhs=a_words[:, n, :].bitcast(FP8X4),
+                        rhs_scale=a_scales[:, n, :],
+                        start=(g == 0),
+                        stop=(g == PASSES - 1),
+                    )
+
+        def copy_first_half(h_open):
+            h_raw = pool.tile([P, PACK, HALF], BF16, tag="h_raw", bufs=1)
+            for j in range(PACK):
+                nc.scalar.copy(out=h_raw[:, j, :], in_=h_open[j][:])
+            return h_raw
+
+        def pack_first_half(h_raw):
+            h_grouped = pool.tile([P, HALF, PACK], BF16, tag="h_grouped", bufs=2, align_bytes=64)
+            nc.vector.tensor_copy(out=h_grouped[:], in_=h_raw[:].rearrange("p j t -> p t j"))
+            nc.vector.quantize_mx(
+                out=h_words[:, 0:HALF].bitcast(FP8X4),
+                scales=h_scales[:, 0:HALF],
+                in_=h_grouped[:].rearrange("p t j -> p (t j)"),
+            )
+
+        def first_matmul_tile(a_packed):
+            a_words, a_scales = a_packed
+            h_sums = psum.tile([P, PACK, P], F32, tag="sums")
+            for j in range(PACK):
+                cols = slice(j * P, (j + 1) * P)
+                for g in range(PASSES):
+                    nc.tensor.matmul_mx(
+                        out=h_sums[:, j, :],
+                        lhsT=v_words[:, g, cols].bitcast(FP8X4),
+                        lhsT_scale=v_scales[:, g, cols],
+                        rhs=a_words[:, g, :].bitcast(FP8X4),
+                        rhs_scale=a_scales[:, g, :],
+                        start=(g == 0),
+                        stop=(g == PASSES - 1),
+                    )
+            h_grouped = pool.tile([P, P, PACK], BF16, tag="h_grouped", bufs=2, align_bytes=64)
+            nc.scalar.copy(out=h_grouped[:], in_=h_sums[:].rearrange("p j t -> p t j"))
+            return h_grouped
+
+        def pack_tile(i, h_grouped):
+            tokens = slice(i * P, (i + 1) * P)
+            nc.vector.quantize_mx(
+                out=h_words[:, tokens].bitcast(FP8X4),
+                scales=h_scales[:, tokens],
+                in_=h_grouped[:].rearrange("p t j -> p (t j)"),
+            )
+
+        s2_rows = consts.tile([P, PAIR], BF16)
+        nc.vector.memset(s2_rows[:].bitcast(F32), 0.0)
+        nc.sync.dma_start(out=s2_rows[0 : 2 * PASSES, :], in_=s2.rearrange("(a w) -> a w", w=PAIR))
+        gain_rows_bf16 = consts.tile([P, P], BF16)
+        nc.vector.memset(gain_rows_bf16[:].bitcast(F32), 0.0)
+
+        v_raws = []
+        x_raws = []
+        for s in range(SLICES):
+            v_raw = big_tile([P, V_PER_SLICE, PACK, RANK], BF16)
+            x_raw = big_tile([P, TILES_PER_HALF, X_COLS], BF16)
+            load_v(v_raw, V_PER_SLICE * s)
+            for part in range(2):
+                tiles = slice(2 * part, 2 * part + 2)
+                nc.sync.dma_start(out=x_raw[:, tiles, :], in_=x_first[:, tiles, s * X_COLS : (s + 1) * X_COLS])
+            load_v(v_raw, V_PER_SLICE * s + 1)
+            v_raws.append(v_raw)
+            x_raws.append(x_raw)
+
+        s2_turned = psum.tile([P, 2, 2, P], F32, tag="turned")
+        nc.tensor.transpose(s2_turned[:, 0, 0, :], s2_rows[:].bitcast(F32), identity[:])
+        s2_words = consts.tile([P, 2 * PASSES], F32)
+        nc.vector.tensor_copy(out=s2_words[:], in_=s2_turned[:, 0, 0, 0 : 2 * PASSES])
+        s2_values = s2_words[:].bitcast(BF16)
+
+        h_open = []
+        for j in range(PACK):
+            h_bank = psum.tile([P, HALF], F32, tag="sums", name="h_bank")
+            h_open.append(h_bank)
+        u_raws = []
+        odd_v = None
+        a_packed = None
+        for s in range(SLICES):
+            if s > 0:
+                pack_v(V_PER_SLICE * s - 1, odd_v)
+            even_v = sign_v(v_raws[s], V_PER_SLICE * s)
+            odd_v = sign_v(v_raws[s], V_PER_SLICE * s + 1)
+            a_grouped = pool.tile([P, V_PER_SLICE, HALF, PACK], BF16, tag="a_grouped", align_bytes=64)
+            for n in range(TILES_PER_HALF):
+                turn_and_scale_x(x_raws[s][:, n, :], V_PER_SLICE * s, a_grouped[:, :, n * P : (n + 1) * P, :])
+            pack_v(V_PER_SLICE * s, even_v)
+            if s > 0:
+                first_matmul_slice(s - 1, a_packed, h_open)
+            a_packed = pack_a(a_grouped, V_PER_SLICE, HALF)
+            u_raws.append(load_u(s))
+            x_raws.append(load_x(TILES_PER_HALF + s))
+        pack_v(PASSES - 1, odd_v)
+
+        nc.sync.dma_start(
+            out=gain_rows_bf16[0:TURNED_TILES, :], in_=s1[0:TURNED_COLS].rearrange("(c p) -> c p", p=P)
+        )
+        nc.sync.dma_start(
+            out=gain_rows_bf16[TURNED_TILES : 2 * TURNED_TILES, :],
+            in_=bias[0:TURNED_COLS].rearrange("(c p) -> c p", p=P),
+        )
+        nc.sync.dma_start(out=s1_spread[:], in_=s1[TURNED_COLS:D_OUT].partition_broadcast(P))
+        nc.sync.dma_start(out=bias_spread[:], in_=bias[TURNED_COLS:D_OUT].partition_broadcast(P))
+
+        u_waiting = None
+        h_waiting = None
+        for s in range(SLICES):
+            a_grouped = pool.tile([P, PASSES, P, PACK], BF16, tag="a_grouped", align_bytes=64)
+            u_grouped = pool.tile([P, U_CHUNK, PACK], BF16, tag="u_grouped", align_bytes=64)
+            for b in range(U_CHUNK // PAIR):
+                turn_and_sign_u(u_raws[s], b, u_grouped)
+                turn_and_scale_x(
+                    x_raws[SLICES + s][:, b * X_COLS : (b + 1) * X_COLS], 2 * b, a_grouped[:, 2 * b : 2 * b + 2, :, :]
                 )
+            if s > 1:
+                pack_tile(TILES_PER_HALF + s - 2, h_waiting)
+            elif s == 1:
+                pack_first_half(h_waiting)
+            if s == 0:
+                first_matmul_slice(SLICES - 1, a_packed, h_open)
+                h_waiting = copy_first_half(h_open)
+            else:
+                pack_u(s - 1, u_waiting)
+                h_waiting = first_matmul_tile(a_packed)
+            a_packed = pack_a(a_grouped, PASSES, P)
+            u_waiting = u_grouped
 
-            s2_rows = first.tile([P, PAIR], BF16)
-            nc.vector.memset(s2_rows[:].bitcast(F32), 0.0)
-            nc.sync.dma_start(out=s2_rows[0 : 2 * PASSES, :], in_=s2.rearrange("(a w) -> a w", w=PAIR))
-            gain_rows_bf16 = first.tile([P, P], BF16)
-            nc.vector.memset(gain_rows_bf16[:].bitcast(F32), 0.0)
-            nc.sync.dma_start(
-                out=gain_rows_bf16[0:TURNED_TILES, :], in_=s1[0:TURNED_COLS].rearrange("(c p) -> c p", p=P)
-            )
-            nc.sync.dma_start(
-                out=gain_rows_bf16[TURNED_TILES : 2 * TURNED_TILES, :],
-                in_=bias[0:TURNED_COLS].rearrange("(c p) -> c p", p=P),
-            )
+        def finish_second_half():
+            pack_tile(TOKEN_TILES - 2, h_waiting)
+            pack_tile(TOKEN_TILES - 1, first_matmul_tile(a_packed))
 
-            v_raws = []
-            x_raws = []
-            u_raws = []
-            for s in range(V_SLICES):
-                v_raws.append(load_v(V_PER_SLICE * s))
-                x_raws.append(load_x(s))
-                v_raws.append(load_v(V_PER_SLICE * s + 1))
+        pack_u(SLICES - 1, u_waiting)
+        gain_rows = consts.tile([P, P], F32)
+        nc.vector.tensor_copy(out=gain_rows[:], in_=gain_rows_bf16[:])
+        gain_turned = psum.tile([P, 2, 2, P], F32, tag="turned")
+        nc.tensor.transpose(gain_turned[:, 0, 0, :], gain_rows[:], identity[:])
+        nc.vector.tensor_copy(out=gain_cols[:], in_=gain_turned[:, 0, 0, 0 : 2 * TURNED_TILES])
 
-            s2_turned = turned.tile([P, 2, 2, P], F32, tag="x_turned")
-            nc.tensor.transpose(s2_turned[:, 0, 0, :], s2_rows[:].bitcast(F32), identity[:])
-            s2_words = first.tile([P, 2 * PASSES], F32)
-            nc.vector.tensor_copy(out=s2_words[:], in_=s2_turned[:, 0, 0, 0 : 2 * PASSES])
-            s2_values = s2_words[:].bitcast(BF16)
-            gain_rows = first.tile([P, P], F32)
-            nc.vector.tensor_copy(out=gain_rows[:], in_=gain_rows_bf16[:])
-            gain_turned = turned.tile([P, 2, 2, P], F32, tag="x_turned")
-            nc.tensor.transpose(gain_turned[:, 0, 0, :], gain_rows[:], identity[:])
-            nc.vector.tensor_copy(out=gain_cols[:], in_=gain_turned[:, 0, 0, 0 : 2 * TURNED_TILES])
+        units_per_block = BLOCK // PAIR
+        units_per_half = TURNED_BLOCKS * units_per_block
+        pieces_per_half = DIRECT_BLOCKS * TILES_PER_HALF
+        units = (TOKENS // HALF) * units_per_half
+        scalar_scaled = 6
 
-            a_packed = []
-            banks = PASSES // 2
+        def spread(unit, count):
+            n = unit % units_per_half
+            return range(n * count // units_per_half, (n + 1) * count // units_per_half)
 
-            odd_v = None
-            for s in range(V_SLICES):
-                if s > 0:
-                    pack_v(V_PER_SLICE * s - 1, odd_v)
-                even_v = sign_v(v_raws[V_PER_SLICE * s])
-                odd_v = sign_v(v_raws[V_PER_SLICE * s + 1])
-                a_grouped = grouped.tile([P, PASSES, P, PACK], BF16, tag="a_grouped", align_bytes=64)
-                for b in range(banks):
-                    turn_and_scale_x(x_raws[s], b, a_grouped)
-                pack_v(V_PER_SLICE * s, even_v)
-                a_packed.append(pack_a(a_grouped))
-                u_raws.append(load_u(s))
-                x_raws.append(load_x(s + V_SLICES))
-            pack_v(PASSES - 1, odd_v)
+        def store(result, half, first_col):
+            token_tiles = slice(half * TILES_PER_HALF, (half + 1) * TILES_PER_HALF)
+            nc.sync.dma_start(out=out_view[:, token_tiles, first_col : first_col + BLOCK], in_=result[:])
 
-            nc.sync.dma_start(out=s1_spread[:], in_=s1[TURNED_COLS:D_OUT].partition_broadcast(P))
-            nc.sync.dma_start(out=bias_spread[:], in_=bias[TURNED_COLS:D_OUT].partition_broadcast(P))
-
-            for s in range(V_SLICES, SLICES):
-                chunk = s - V_SLICES
-                a_grouped = grouped.tile([P, PASSES, P, PACK], BF16, tag="a_grouped", align_bytes=64)
-                u_grouped = grouped.tile([P, U_CHUNK, PACK], BF16, tag="u_grouped", align_bytes=64)
-                for b in range(banks):
-                    turn_and_sign_u(u_raws[chunk], b, u_grouped)
-                    turn_and_scale_x(x_raws[s], b, a_grouped)
-                a_packed.append(pack_a(a_grouped))
-                pack_u(chunk, u_grouped)
-                for i in range(2 * chunk, 2 * chunk + 2):
-                    first_matmul(i, a_packed[i][0], a_packed[i][1])
-
-        with ExitStack() as phase2:
-            scaled = phase2.enter_context(tc.tile_pool(name="scaled", bufs=4, reuse_waits="tile"))
-            results = phase2.enter_context(tc.tile_pool(name="results", bufs=3, reuse_waits="tile"))
-            products = phase2.enter_context(tc.psum_pool(name="products", bufs=2, reuse_waits="tile"))
-            back = phase2.enter_context(tc.psum_pool(name="back", bufs=4, reuse_waits="tile"))
-
-            units_per_block = 2
-            blocks = TURNED_COLS // BLOCK
-            units = (TOKENS // HALF) * blocks * units_per_block
-
-            def place(unit):
-                half, rest = divmod(unit, blocks * units_per_block)
-                block, part = divmod(rest, units_per_block)
-                return half, block, part
-
-            def store(result, half, first_col):
-                token_tiles = slice(half * TILES_PER_HALF, (half + 1) * TILES_PER_HALF)
-                nc.sync.dma_start(out=out_view[:, token_tiles, first_col : first_col + BLOCK], in_=result[:])
-
-            def start_turned(unit):
-                half, block, part = place(unit)
-                tokens = slice(half * HALF, (half + 1) * HALF)
-                z_tiles = []
-                for j in range(2):
-                    c = (block * units_per_block + part) * 2 + j
-                    z_sums = products.tile([P, HALF], F32, tag="z_sums")
-                    nc.tensor.matmul_mx(
-                        out=z_sums[:],
-                        lhsT=u_words[:, c * P : (c + 1) * P].bitcast(FP8X4),
-                        lhsT_scale=u_scales[:, c * P : (c + 1) * P],
-                        rhs=h_words[:, tokens].bitcast(FP8X4),
-                        rhs_scale=h_scales[:, tokens],
-                        start=True,
-                        stop=True,
-                    )
-                    z_tile = scaled.tile([P, HALF], F32, tag="z_tile")
+        def start_turned(unit):
+            half, n = divmod(unit, units_per_half)
+            tokens = slice(half * HALF, (half + 1) * HALF)
+            z_tiles = []
+            for j in range(2):
+                c = 2 * n + j
+                gain = gain_cols[:, c : c + 1]
+                offset = gain_cols[:, TURNED_TILES + c : TURNED_TILES + c + 1]
+                z_sums = psum.tile([P, HALF], F32, tag="sums")
+                nc.tensor.matmul_mx(
+                    out=z_sums[:],
+                    lhsT=u_words[:, c * P : (c + 1) * P].bitcast(FP8X4),
+                    lhsT_scale=u_scales[:, c * P : (c + 1) * P],
+                    rhs=h_words[:, tokens].bitcast(FP8X4),
+                    rhs_scale=h_scales[:, tokens],
+                    start=True,
+                    stop=True,
+                )
+                z_tile = pool.tile([P, HALF], F32, tag="z_tile", bufs=4)
+                if j == 1 and len(spread(unit, scalar_scaled)) > 0:
+                    nc.scalar.activation(out=z_tile[:], in_=z_sums[:], func=IDENTITY, scale=gain, bias=offset)
+                else:
                     nc.vector.tensor_scalar(
-                        out=z_tile[:],
-                        in0=z_sums[:],
-                        scalar1=gain_cols[:, c : c + 1],
-                        scalar2=gain_cols[:, TURNED_TILES + c : TURNED_TILES + c + 1],
-                        op0=MULT,
-                        op1=ADD,
+                        out=z_tile[:], in0=z_sums[:], scalar1=gain, scalar2=offset, op0=MULT, op1=ADD
                     )
-                    z_tiles.append(z_tile)
-                return z_tiles
+                z_tiles.append(z_tile)
+            return z_tiles
 
-            def finish_turned(unit, z_tiles, result):
-                first_col = place(unit)[2] * PAIR
-                for a in range(TILES_PER_HALF // 2):
-                    z_back = back.tile([P, 2, PAIR], F32, tag="z_back")
-                    for i in range(2):
-                        tokens = slice((2 * a + i) * P, (2 * a + i + 1) * P)
-                        for j in range(2):
-                            nc.tensor.transpose(z_back[:, i, j * P : (j + 1) * P], z_tiles[j][:, tokens], identity[:])
-                    nc.scalar.copy(out=result[:, 2 * a : 2 * a + 2, first_col : first_col + PAIR], in_=z_back[:])
+        def finish_turned(unit, z_tiles, result):
+            first_col = unit % units_per_block * PAIR
+            for a in range(TILES_PER_HALF // 2):
+                z_back = psum.tile([P, 2, PAIR], F32, tag="turned")
+                for i in range(2):
+                    tokens = slice((2 * a + i) * P, (2 * a + i + 1) * P)
+                    for j in range(2):
+                        nc.tensor.transpose(z_back[:, i, j * P : (j + 1) * P], z_tiles[j][:, tokens], identity[:])
+                nc.scalar.copy(out=result[:, 2 * a : 2 * a + 2, first_col : first_col + PAIR], in_=z_back[:])
 
-            def direct(unit, result):
-                half, block, part = place(unit)
-                cols = slice(block * BLOCK, (block + 1) * BLOCK)
-                u_cols = slice(TURNED_COLS + block * BLOCK, TURNED_COLS + (block + 1) * BLOCK)
-                for j in range(2):
-                    i = 2 * part + j
-                    tokens = slice((half * TILES_PER_HALF + i) * P, (half * TILES_PER_HALF + i + 1) * P)
-                    z_direct = products.tile([P, BLOCK], F32, tag="z_direct")
-                    nc.tensor.matmul_mx(
-                        out=z_direct[:],
-                        lhsT=h_words[:, tokens].bitcast(FP8X4),
-                        lhsT_scale=h_scales[:, tokens],
-                        rhs=u_words[:, u_cols].bitcast(FP8X4),
-                        rhs_scale=u_scales[:, u_cols],
-                        start=True,
-                        stop=True,
-                    )
-                    z_gained = scaled.tile([P, BLOCK], F32, tag="z_gained")
-                    nc.vector.tensor_tensor(out=z_gained[:], in0=z_direct[:], in1=s1_spread[:, cols], op=MULT)
-                    nc.gpsimd.tensor_tensor(out=result[:, i, :], in0=z_gained[:], in1=bias_spread[:, cols], op=ADD)
+        def direct(half, piece, result):
+            block, i = divmod(piece, TILES_PER_HALF)
+            cols = slice(block * BLOCK, (block + 1) * BLOCK)
+            u_cols = slice(TURNED_COLS + block * BLOCK, TURNED_COLS + (block + 1) * BLOCK)
+            tokens = slice((half * TILES_PER_HALF + i) * P, (half * TILES_PER_HALF + i + 1) * P)
+            z_direct = psum.tile([P, BLOCK], F32, tag="sums")
+            nc.tensor.matmul_mx(
+                out=z_direct[:],
+                lhsT=h_words[:, tokens].bitcast(FP8X4),
+                lhsT_scale=h_scales[:, tokens],
+                rhs=u_words[:, u_cols].bitcast(FP8X4),
+                rhs_scale=u_scales[:, u_cols],
+                start=True,
+                stop=True,
+            )
+            z_gained = pool.tile([P, BLOCK], F32, tag="z_gained", bufs=4)
+            nc.vector.tensor_tensor(out=z_gained[:], in0=z_direct[:], in1=s1_spread[:, cols], op=MULT)
+            nc.gpsimd.tensor_tensor(out=result[:, i, :], in0=z_gained[:], in1=bias_spread[:, cols], op=ADD)
 
-            result_turned = None
-            result_direct = None
-            waiting = None
-            for unit in range(-1, units):
-                ready = waiting
-                if unit + 1 < units:
-                    waiting = start_turned(unit + 1)
-                if unit >= 0:
-                    half, block, part = place(unit)
-                    if part == 0:
-                        result_turned = results.tile([P, TILES_PER_HALF, BLOCK], F32, tag="result_turned")
-                    finish_turned(unit, ready, result_turned)
-                    if part == units_per_block - 1:
-                        store(result_turned, half, block * BLOCK)
-                if unit + 1 < units:
-                    half, block, part = place(unit + 1)
-                    if part == 0:
-                        result_direct = results.tile([P, TILES_PER_HALF, BLOCK], F32, tag="result_direct")
-                    direct(unit + 1, result_direct)
-                    if part == units_per_block - 1:
+        result_turned = None
+        result_direct = None
+        waiting = None
+        for unit in range(-1, units):
+            ready = waiting
+            if unit == 1:
+                finish_second_half()
+            if unit + 1 < units:
+                waiting = start_turned(unit + 1)
+            if unit >= 0:
+                half, n = divmod(unit, units_per_half)
+                block, part = divmod(n, units_per_block)
+                if part == 0:
+                    result_turned = big_tile([P, TILES_PER_HALF, BLOCK], F32)
+                finish_turned(unit, ready, result_turned)
+                if part == units_per_block - 1:
+                    store(result_turned, half, block * BLOCK)
+            if unit + 1 < units:
+                half = (unit + 1) // units_per_half
+                for piece in spread(unit + 1, pieces_per_half):
+                    block, i = divmod(piece, TILES_PER_HALF)
+                    if i == 0:
+                        result_direct = big_tile([P, TILES_PER_HALF, BLOCK], F32)
+                    direct(half, piece, result_direct)
+                    if i == TILES_PER_HALF - 1:
                         store(result_direct, half, TURNED_COLS + block * BLOCK)

@@ -33,11 +33,9 @@ X_COLS = V_PER_SLICE * K_PASS
 U_CHUNK = D_OUT // SLICES
 PAIR = 2 * P
 
-BLOCK = BANK
-TURNED_BLOCKS = 5
-TURNED_COLS = TURNED_BLOCKS * BLOCK
-TURNED_TILES = TURNED_COLS // P
-DIRECT_BLOCKS = D_OUT // BLOCK - TURNED_BLOCKS
+CHANNEL_TILES = D_OUT // P
+BLOCK = U_CHUNK // 2
+STEPS = U_CHUNK // PAIR
 
 FLOPS = 2 * TOKENS * D_IN * RANK + 2 * TOKENS * RANK * D_OUT
 
@@ -65,9 +63,9 @@ def tile_binaryfactoredlinear_pa_kernel(tc, x, U_latent, V_latent, s1, s2, bias,
         u_scales = consts.tile([P, D_OUT], U8, align_bytes=64)
         h_words = consts.tile([P, TOKENS], U32, align_bytes=64)
         h_scales = consts.tile([P, TOKENS], U8, align_bytes=64)
-        gain_cols = consts.tile([P, 2 * TURNED_TILES], F32)
-        s1_spread = consts.tile([P, D_OUT - TURNED_COLS], BF16)
-        bias_spread = consts.tile([P, D_OUT - TURNED_COLS], BF16)
+        gain_cols = consts.tile([P, 2 * CHANNEL_TILES], F32)
+        s1_spread = consts.tile([P, SLICES, BLOCK], BF16)
+        bias_spread = consts.tile([P, SLICES, BLOCK], BF16)
 
         def big_tile(shape, dtype):
             tile = pool.tile(shape, dtype, tag="big", bufs=10, name="big")
@@ -156,55 +154,34 @@ def tile_binaryfactoredlinear_pa_kernel(tc, x, U_latent, V_latent, s1, s2, bias,
             )
             return a_words, a_scales
 
-        def first_matmul_slice(s, a_packed, h_open):
+        def first_matmul_pass(g, a_packed, h_banks):
             a_words, a_scales = a_packed
-            for n in range(V_PER_SLICE):
-                g = V_PER_SLICE * s + n
-                for j in range(PACK):
-                    cols = slice(j * P, (j + 1) * P)
-                    nc.tensor.matmul_mx(
-                        out=h_open[j][:],
-                        lhsT=v_words[:, g, cols].bitcast(FP8X4),
-                        lhsT_scale=v_scales[:, g, cols],
-                        rhs=a_words[:, n, :].bitcast(FP8X4),
-                        rhs_scale=a_scales[:, n, :],
-                        start=(g == 0),
-                        stop=(g == PASSES - 1),
-                    )
-
-        def copy_first_half(h_open):
-            h_raw = pool.tile([P, PACK, HALF], BF16, tag="h_raw", bufs=1)
-            for j in range(PACK):
-                nc.scalar.copy(out=h_raw[:, j, :], in_=h_open[j][:])
-            return h_raw
-
-        def pack_first_half(h_raw):
-            h_grouped = pool.tile([P, HALF, PACK], BF16, tag="h_grouped", bufs=2, align_bytes=64)
-            nc.vector.tensor_copy(out=h_grouped[:], in_=h_raw[:].rearrange("p j t -> p t j"))
-            nc.vector.quantize_mx(
-                out=h_words[:, 0:HALF].bitcast(FP8X4),
-                scales=h_scales[:, 0:HALF],
-                in_=h_grouped[:].rearrange("p t j -> p (t j)"),
-            )
-
-        def first_matmul_tile(a_packed):
-            a_words, a_scales = a_packed
-            h_sums = psum.tile([P, PACK, P], F32, tag="sums")
-            for j in range(PACK):
+            n = g % V_PER_SLICE
+            for j, h_bank in h_banks:
                 cols = slice(j * P, (j + 1) * P)
-                for g in range(PASSES):
-                    nc.tensor.matmul_mx(
-                        out=h_sums[:, j, :],
-                        lhsT=v_words[:, g, cols].bitcast(FP8X4),
-                        lhsT_scale=v_scales[:, g, cols],
-                        rhs=a_words[:, g, :].bitcast(FP8X4),
-                        rhs_scale=a_scales[:, g, :],
-                        start=(g == 0),
-                        stop=(g == PASSES - 1),
-                    )
-            h_grouped = pool.tile([P, P, PACK], BF16, tag="h_grouped", bufs=2, align_bytes=64)
-            nc.scalar.copy(out=h_grouped[:], in_=h_sums[:].rearrange("p j t -> p t j"))
-            return h_grouped
+                nc.tensor.matmul_mx(
+                    out=h_bank[:],
+                    lhsT=v_words[:, g, cols].bitcast(FP8X4),
+                    lhsT_scale=v_scales[:, g, cols],
+                    rhs=a_words[:, n, :].bitcast(FP8X4),
+                    rhs_scale=a_scales[:, n, :],
+                    start=(g == 0),
+                    stop=(g == PASSES - 1),
+                )
+
+        def first_matmul_group(j, a_packed, h_sums):
+            a_words, a_scales = a_packed
+            cols = slice(j * P, (j + 1) * P)
+            for g in range(PASSES):
+                nc.tensor.matmul_mx(
+                    out=h_sums[:, j, :],
+                    lhsT=v_words[:, g, cols].bitcast(FP8X4),
+                    lhsT_scale=v_scales[:, g, cols],
+                    rhs=a_words[:, g, :].bitcast(FP8X4),
+                    rhs_scale=a_scales[:, g, :],
+                    start=(g == 0),
+                    stop=(g == PASSES - 1),
+                )
 
         def pack_tile(i, h_grouped):
             tokens = slice(i * P, (i + 1) * P)
@@ -241,8 +218,9 @@ def tile_binaryfactoredlinear_pa_kernel(tc, x, U_latent, V_latent, s1, s2, bias,
 
         h_open = []
         for j in range(PACK):
-            h_bank = psum.tile([P, HALF], F32, tag="sums", name="h_bank")
-            h_open.append(h_bank)
+            tag = "h" if j == PACK - 1 else "sums"
+            h_bank = psum.tile([P, HALF], F32, tag=tag, bufs=1 if j == PACK - 1 else 3, name="h_bank")
+            h_open.append((j, h_bank))
         u_raws = []
         odd_v = None
         a_packed = None
@@ -254,116 +232,66 @@ def tile_binaryfactoredlinear_pa_kernel(tc, x, U_latent, V_latent, s1, s2, bias,
             a_grouped = pool.tile([P, V_PER_SLICE, HALF, PACK], BF16, tag="a_grouped", align_bytes=64)
             for n in range(TILES_PER_HALF):
                 turn_and_scale_x(x_raws[s][:, n, :], V_PER_SLICE * s, a_grouped[:, :, n * P : (n + 1) * P, :])
+                if s > 0 and n % 2 == 1:
+                    first_matmul_pass(V_PER_SLICE * (s - 1) + n // 2, a_packed, h_open)
             pack_v(V_PER_SLICE * s, even_v)
-            if s > 0:
-                first_matmul_slice(s - 1, a_packed, h_open)
             a_packed = pack_a(a_grouped, V_PER_SLICE, HALF)
             u_raws.append(load_u(s))
             x_raws.append(load_x(TILES_PER_HALF + s))
+            if s == 0:
+                for row, vector in enumerate((s1, bias)):
+                    nc.sync.dma_start(
+                        out=gain_rows_bf16[row * CHANNEL_TILES : (row + 1) * CHANNEL_TILES, :],
+                        in_=vector.rearrange("(c p) -> c p", p=P),
+                    )
+            direct_channels = slice(s * U_CHUNK + BLOCK, (s + 1) * U_CHUNK)
+            nc.sync.dma_start(out=s1_spread[:, s, :], in_=s1[direct_channels].partition_broadcast(P))
+            nc.sync.dma_start(out=bias_spread[:, s, :], in_=bias[direct_channels].partition_broadcast(P))
         pack_v(PASSES - 1, odd_v)
 
-        nc.sync.dma_start(
-            out=gain_rows_bf16[0:TURNED_TILES, :], in_=s1[0:TURNED_COLS].rearrange("(c p) -> c p", p=P)
-        )
-        nc.sync.dma_start(
-            out=gain_rows_bf16[TURNED_TILES : 2 * TURNED_TILES, :],
-            in_=bias[0:TURNED_COLS].rearrange("(c p) -> c p", p=P),
-        )
-        nc.sync.dma_start(out=s1_spread[:], in_=s1[TURNED_COLS:D_OUT].partition_broadcast(P))
-        nc.sync.dma_start(out=bias_spread[:], in_=bias[TURNED_COLS:D_OUT].partition_broadcast(P))
+        def turn_gains():
+            gain_rows = consts.tile([P, P], F32)
+            nc.vector.tensor_copy(out=gain_rows[:], in_=gain_rows_bf16[:])
+            gain_turned = psum.tile([P, 2, 2, P], F32, tag="turned")
+            nc.tensor.transpose(gain_turned[:, 0, 0, :], gain_rows[:], identity[:])
+            nc.vector.tensor_copy(out=gain_cols[:], in_=gain_turned[:, 0, 0, 0 : 2 * CHANNEL_TILES])
 
-        u_waiting = None
-        h_waiting = None
-        for s in range(SLICES):
-            a_grouped = pool.tile([P, PASSES, P, PACK], BF16, tag="a_grouped", align_bytes=64)
-            u_grouped = pool.tile([P, U_CHUNK, PACK], BF16, tag="u_grouped", align_bytes=64)
-            for b in range(U_CHUNK // PAIR):
-                turn_and_sign_u(u_raws[s], b, u_grouped)
-                turn_and_scale_x(
-                    x_raws[SLICES + s][:, b * X_COLS : (b + 1) * X_COLS], 2 * b, a_grouped[:, 2 * b : 2 * b + 2, :, :]
-                )
-            if s > 1:
-                pack_tile(TILES_PER_HALF + s - 2, h_waiting)
-            elif s == 1:
-                pack_first_half(h_waiting)
-            if s == 0:
-                first_matmul_slice(SLICES - 1, a_packed, h_open)
-                h_waiting = copy_first_half(h_open)
-            else:
-                pack_u(s - 1, u_waiting)
-                h_waiting = first_matmul_tile(a_packed)
-            a_packed = pack_a(a_grouped, PASSES, P)
-            u_waiting = u_grouped
-
-        def finish_second_half():
-            pack_tile(TOKEN_TILES - 2, h_waiting)
-            pack_tile(TOKEN_TILES - 1, first_matmul_tile(a_packed))
-
-        pack_u(SLICES - 1, u_waiting)
-        gain_rows = consts.tile([P, P], F32)
-        nc.vector.tensor_copy(out=gain_rows[:], in_=gain_rows_bf16[:])
-        gain_turned = psum.tile([P, 2, 2, P], F32, tag="turned")
-        nc.tensor.transpose(gain_turned[:, 0, 0, :], gain_rows[:], identity[:])
-        nc.vector.tensor_copy(out=gain_cols[:], in_=gain_turned[:, 0, 0, 0 : 2 * TURNED_TILES])
-
-        units_per_block = BLOCK // PAIR
-        units_per_half = TURNED_BLOCKS * units_per_block
-        pieces_per_half = DIRECT_BLOCKS * TILES_PER_HALF
-        units = (TOKENS // HALF) * units_per_half
-        scalar_scaled = 6
-
-        def spread(unit, count):
-            n = unit % units_per_half
-            return range(n * count // units_per_half, (n + 1) * count // units_per_half)
-
-        def store(result, half, first_col):
-            token_tiles = slice(half * TILES_PER_HALF, (half + 1) * TILES_PER_HALF)
-            nc.sync.dma_start(out=out_view[:, token_tiles, first_col : first_col + BLOCK], in_=result[:])
-
-        def start_turned(unit):
-            half, n = divmod(unit, units_per_half)
+        def start_turned(half, i):
+            chunk, tile = divmod(i, STEPS)
+            c = chunk * (U_CHUNK // P) + tile
             tokens = slice(half * HALF, (half + 1) * HALF)
-            z_tiles = []
-            for j in range(2):
-                c = 2 * n + j
-                gain = gain_cols[:, c : c + 1]
-                offset = gain_cols[:, TURNED_TILES + c : TURNED_TILES + c + 1]
-                z_sums = psum.tile([P, HALF], F32, tag="sums")
-                nc.tensor.matmul_mx(
-                    out=z_sums[:],
-                    lhsT=u_words[:, c * P : (c + 1) * P].bitcast(FP8X4),
-                    lhsT_scale=u_scales[:, c * P : (c + 1) * P],
-                    rhs=h_words[:, tokens].bitcast(FP8X4),
-                    rhs_scale=h_scales[:, tokens],
-                    start=True,
-                    stop=True,
-                )
-                z_tile = pool.tile([P, HALF], F32, tag="z_tile", bufs=4)
-                if j == 1 and len(spread(unit, scalar_scaled)) > 0:
-                    nc.scalar.activation(out=z_tile[:], in_=z_sums[:], func=IDENTITY, scale=gain, bias=offset)
-                else:
-                    nc.vector.tensor_scalar(
-                        out=z_tile[:], in0=z_sums[:], scalar1=gain, scalar2=offset, op0=MULT, op1=ADD
-                    )
-                z_tiles.append(z_tile)
-            return z_tiles
+            gain = gain_cols[:, c : c + 1]
+            offset = gain_cols[:, CHANNEL_TILES + c : CHANNEL_TILES + c + 1]
+            z_sums = psum.tile([P, HALF], F32, tag="sums", bufs=3)
+            nc.tensor.matmul_mx(
+                out=z_sums[:],
+                lhsT=u_words[:, c * P : (c + 1) * P].bitcast(FP8X4),
+                lhsT_scale=u_scales[:, c * P : (c + 1) * P],
+                rhs=h_words[:, tokens].bitcast(FP8X4),
+                rhs_scale=h_scales[:, tokens],
+                start=True,
+                stop=True,
+            )
+            z_tile = pool.tile([P, HALF], F32, tag="z_tile", bufs=7)
+            if tile % 2 == 0:
+                nc.vector.tensor_scalar(out=z_tile[:], in0=z_sums[:], scalar1=gain, scalar2=offset, op0=MULT, op1=ADD)
+            else:
+                nc.scalar.activation(out=z_tile[:], in_=z_sums[:], func=IDENTITY, scale=gain, bias=offset)
+            return z_tile
 
-        def finish_turned(unit, z_tiles, result):
-            first_col = unit % units_per_block * PAIR
-            for a in range(TILES_PER_HALF // 2):
-                z_back = psum.tile([P, 2, PAIR], F32, tag="turned")
-                for i in range(2):
-                    tokens = slice((2 * a + i) * P, (2 * a + i + 1) * P)
-                    for j in range(2):
-                        nc.tensor.transpose(z_back[:, i, j * P : (j + 1) * P], z_tiles[j][:, tokens], identity[:])
-                nc.scalar.copy(out=result[:, 2 * a : 2 * a + 2, first_col : first_col + PAIR], in_=z_back[:])
+        def turn_back(z_pair, a, first_col, result):
+            z_back = psum.tile([P, 2, PAIR], F32, tag="turned")
+            for n in range(2):
+                tokens = slice((2 * a + n) * P, (2 * a + n + 1) * P)
+                for j in range(2):
+                    nc.tensor.transpose(z_back[:, n, j * P : (j + 1) * P], z_pair[j][:, tokens], identity[:])
+            nc.scalar.copy(out=result[:, 2 * a : 2 * a + 2, first_col : first_col + PAIR], in_=z_back[:])
 
-        def direct(half, piece, result):
-            block, i = divmod(piece, TILES_PER_HALF)
-            cols = slice(block * BLOCK, (block + 1) * BLOCK)
-            u_cols = slice(TURNED_COLS + block * BLOCK, TURNED_COLS + (block + 1) * BLOCK)
-            tokens = slice((half * TILES_PER_HALF + i) * P, (half * TILES_PER_HALF + i + 1) * P)
-            z_direct = psum.tile([P, BLOCK], F32, tag="sums")
+        def direct(half, i, result):
+            chunk, tile = divmod(i, STEPS)
+            u_cols = slice(chunk * U_CHUNK + BLOCK, (chunk + 1) * U_CHUNK)
+            tokens = slice((half * TILES_PER_HALF + tile) * P, (half * TILES_PER_HALF + tile + 1) * P)
+            z_direct = psum.tile([P, BLOCK], F32, tag="sums", bufs=3)
             nc.tensor.matmul_mx(
                 out=z_direct[:],
                 lhsT=h_words[:, tokens].bitcast(FP8X4),
@@ -374,32 +302,98 @@ def tile_binaryfactoredlinear_pa_kernel(tc, x, U_latent, V_latent, s1, s2, bias,
                 stop=True,
             )
             z_gained = pool.tile([P, BLOCK], F32, tag="z_gained", bufs=4)
-            nc.vector.tensor_tensor(out=z_gained[:], in0=z_direct[:], in1=s1_spread[:, cols], op=MULT)
-            nc.gpsimd.tensor_tensor(out=result[:, i, :], in0=z_gained[:], in1=bias_spread[:, cols], op=ADD)
+            nc.vector.tensor_tensor(out=z_gained[:], in0=z_direct[:], in1=s1_spread[:, chunk, :], op=MULT)
+            nc.gpsimd.tensor_tensor(out=result[:, tile, :], in0=z_gained[:], in1=bias_spread[:, chunk, :], op=ADD)
 
+        pieces = SLICES * STEPS
+        GROUP_LAG = STEPS + 2
+        LAG = 7
+        BACK_LAG = 4
+        u_grouped = None
+        a_grouped = None
+        u_waiting = None
+        h_raw = None
+        h_sums = None
+        h_grouped = None
+        second_packed = []
+        z_tiles = {}
         result_turned = None
         result_direct = None
-        waiting = None
-        for unit in range(-1, units):
-            ready = waiting
-            if unit == 1:
-                finish_second_half()
-            if unit + 1 < units:
-                waiting = start_turned(unit + 1)
-            if unit >= 0:
-                half, n = divmod(unit, units_per_half)
-                block, part = divmod(n, units_per_block)
-                if part == 0:
+        for k in range(LAG + 2 * pieces + BACK_LAG):
+            s, b = divmod(k, STEPS)
+            m = k - LAG
+            group = k - GROUP_LAG
+            if k < pieces:
+                if b == 0:
+                    a_ready = a_grouped
+                    u_waiting = u_grouped
+                    a_grouped = pool.tile([P, PASSES, P, PACK], BF16, tag="a_grouped", align_bytes=64)
+                    u_grouped = pool.tile([P, U_CHUNK, PACK], BF16, tag="u_grouped", align_bytes=64)
+                turn_and_sign_u(u_raws[s], b, u_grouped)
+                turn_and_scale_x(
+                    x_raws[SLICES + s][:, b * X_COLS : (b + 1) * X_COLS], 2 * b, a_grouped[:, 2 * b : 2 * b + 2, :, :]
+                )
+            elif k == pieces:
+                a_ready = a_grouped
+                u_waiting = u_grouped
+            back = m - BACK_LAG
+            if back >= 0:
+                half, i = divmod(back, pieces)
+                chunk, rest = divmod(i, STEPS)
+                unit, a = divmod(rest, 2)
+                if rest == 0:
                     result_turned = big_tile([P, TILES_PER_HALF, BLOCK], F32)
-                finish_turned(unit, ready, result_turned)
-                if part == units_per_block - 1:
-                    store(result_turned, half, block * BLOCK)
-            if unit + 1 < units:
-                half = (unit + 1) // units_per_half
-                for piece in spread(unit + 1, pieces_per_half):
-                    block, i = divmod(piece, TILES_PER_HALF)
-                    if i == 0:
-                        result_direct = big_tile([P, TILES_PER_HALF, BLOCK], F32)
-                    direct(half, piece, result_direct)
-                    if i == TILES_PER_HALF - 1:
-                        store(result_direct, half, TURNED_COLS + block * BLOCK)
+                turn_back((z_tiles[back - a], z_tiles[back - a + 1]), a, unit * PAIR, result_turned)
+                if a == 1:
+                    columns = slice(unit * PAIR, (unit + 1) * PAIR)
+                    channels = slice(chunk * U_CHUNK + unit * PAIR, chunk * U_CHUNK + (unit + 1) * PAIR)
+                    nc.sync.dma_start(
+                        out=out_view[:, half * TILES_PER_HALF : (half + 1) * TILES_PER_HALF, channels],
+                        in_=result_turned[:, :, columns],
+                    )
+            if k == STEPS - 1:
+                turn_gains()
+            if k < PACK:
+                first_matmul_pass(PASSES - V_PER_SLICE + k // 2, a_packed, h_open[2 * (k % 2) : 2 * (k % 2) + 2])
+            if 0 <= group < pieces:
+                j = group % PACK
+                if j == 0:
+                    h_sums = psum.tile([P, PACK, P], F32, tag="h", bufs=1)
+                first_matmul_group(j, second_packed[group // PACK], h_sums)
+            if 0 <= m < 2 * pieces:
+                half, i = divmod(m, pieces)
+                chunk, tile = divmod(i, STEPS)
+                z_tiles[m] = start_turned(half, i)
+                if tile == 0:
+                    result_direct = big_tile([P, TILES_PER_HALF, BLOCK], F32)
+                direct(half, i, result_direct)
+                if tile % 2 == 1:
+                    first_channel = chunk * U_CHUNK + BLOCK
+                    first_tile = half * TILES_PER_HALF + tile - 1
+                    nc.sync.dma_start(
+                        out=out_view[:, first_tile : first_tile + 2, first_channel : first_channel + BLOCK],
+                        in_=result_direct[:, tile - 1 : tile + 1, :],
+                    )
+            if k == PACK:
+                h_raw = pool.tile([P, PACK, HALF], BF16, tag="h_raw", bufs=1)
+                for j, h_bank in h_open:
+                    nc.scalar.copy(out=h_raw[:, j, :], in_=h_bank[:])
+            if k == PACK + 1:
+                h_grouped = pool.tile([P, HALF, PACK], BF16, tag="h_grouped", align_bytes=64)
+                nc.vector.tensor_copy(out=h_grouped[:], in_=h_raw[:].rearrange("p j t -> p t j"))
+            if k == PACK + 2:
+                nc.vector.quantize_mx(
+                    out=h_words[:, 0:HALF].bitcast(FP8X4),
+                    scales=h_scales[:, 0:HALF],
+                    in_=h_grouped[:].rearrange("p t j -> p (t j)"),
+                )
+            if 0 < s <= SLICES:
+                if b == 0:
+                    second_packed.append(pack_a(a_ready, PASSES, P))
+                elif b == 1:
+                    pack_u(s - 1, u_waiting)
+            if 0 < group <= pieces and group % PACK == 0:
+                pack_tile(TILES_PER_HALF + group // PACK - 1, h_grouped)
+            if 0 <= group < pieces and group % PACK == PACK - 1:
+                h_grouped = pool.tile([P, P, PACK], BF16, tag="h_grouped", align_bytes=64)
+                nc.scalar.copy(out=h_grouped[:], in_=h_sums[:].rearrange("p j t -> p t j"))

@@ -34,8 +34,24 @@ U_CHUNK = D_OUT // SLICES
 PAIR = 2 * P
 
 CHANNEL_TILES = D_OUT // P
-BLOCK = U_CHUNK // 2
 STEPS = U_CHUNK // PAIR
+TURNED = (2 * PAIR, 2 * PAIR)
+DIRECT = U_CHUNK - min(TURNED)
+
+BANKS = {
+    "first x": (0, 1, 2, 3),
+    "first h": (4, 5, 6, 7),
+    "first u": (0, 1, 2, 3),
+    "x": (0, 1),
+    "u": (2, 3),
+    "back": (4,),
+    "z": (5,),
+    "d": (6,),
+    "h": (7,),
+    "late back": (0, 1, 2, 3),
+    "late z": (4, 5),
+    "late d": (6, 7),
+}
 
 FLOPS = 2 * TOKENS * D_IN * RANK + 2 * TOKENS * RANK * D_OUT
 
@@ -45,7 +61,7 @@ def tile_binaryfactoredlinear_pa_kernel(tc, x, U_latent, V_latent, s1, s2, bias,
     x_rows = x.flatten_outer_dims()
     x_first = x_rows[0:HALF, :].rearrange("(n p) k -> p n k", p=P)
     v_view = V_latent.rearrange("(g u p e) r -> p g u (e r)", g=PASSES, u=2, p=P, e=2)
-    u_view = U_latent.rearrange("(c p) r -> p c r", p=P)
+    u_view = U_latent.rearrange("(c p t) r -> p c (t r)", c=SLICES, p=P)
     out_view = out.flatten_outer_dims().rearrange("(n p) o -> p n o", p=P)
 
     with ExitStack() as stack:
@@ -64,11 +80,19 @@ def tile_binaryfactoredlinear_pa_kernel(tc, x, U_latent, V_latent, s1, s2, bias,
         h_words = consts.tile([P, TOKENS], U32, align_bytes=64)
         h_scales = consts.tile([P, TOKENS], U8, align_bytes=64)
         gain_cols = consts.tile([P, 2 * CHANNEL_TILES], F32)
-        s1_spread = consts.tile([P, SLICES, BLOCK], BF16)
-        bias_spread = consts.tile([P, SLICES, BLOCK], BF16)
+        s1_spread = consts.tile([P, SLICES, DIRECT], BF16)
+        bias_spread = consts.tile([P, SLICES, DIRECT], BF16)
 
         def big_tile(shape, dtype):
             tile = pool.tile(shape, dtype, tag="big", bufs=10, name="big")
+            return tile
+
+        turn = {}
+
+        def bank(shape, dtype, role):
+            numbers = BANKS[role]
+            turn[role] = turn.get(role, -1) + 1
+            tile = psum.tile(shape, dtype, tag="bank%d" % numbers[turn[role] % len(numbers)], bufs=1, name="bank")
             return tile
 
         def load_v(v_raw, g):
@@ -77,9 +101,8 @@ def tile_binaryfactoredlinear_pa_kernel(tc, x, U_latent, V_latent, s1, s2, bias,
             )
 
         def load_u(chunk):
-            tiles = U_CHUNK // P
-            u_raw = big_tile([P, tiles, RANK], BF16)
-            nc.sync.dma_start(out=u_raw[:], in_=u_view[:, chunk * tiles : (chunk + 1) * tiles, :])
+            u_raw = big_tile([P, U_CHUNK // P, RANK], BF16)
+            nc.sync.dma_start(out=u_raw[:].rearrange("p t r -> p (t r)"), in_=u_view[:, chunk, :])
             return u_raw
 
         def load_x(i):
@@ -105,19 +128,18 @@ def tile_binaryfactoredlinear_pa_kernel(tc, x, U_latent, V_latent, s1, s2, bias,
                 in_=v_grouped[:].rearrange("p c j -> p (c j)"),
             )
 
-        def turn_and_sign_u(u_raw, b, u_grouped):
-            u_turned = psum.tile([P, 2, PAIR], F32, tag="turned")
-            for u in range(2):
-                for j in range(2):
+        def turn_and_sign_u(u_raw, b, u_grouped, role):
+            u_turned = bank([P, 2 * 2, P], F32, role)
+            for t in range(2):
+                for u in range(2):
                     nc.tensor.transpose(
-                        u_turned[:, u, j * P : (j + 1) * P],
-                        u_raw[:, 2 * b + j, :].bitcast(F32)[:, u * P : (u + 1) * P],
+                        u_turned[:, 2 * t + u, :],
+                        u_raw[:, 2 * b + t, :].bitcast(F32)[:, u * P : (u + 1) * P],
                         identity[:],
                     )
+            pairs = u_grouped[:].rearrange("p (q t) (u e) -> p q (t u) e", q=P, u=2)[:, :, 4 * b : 4 * b + 4, :]
             nc.scalar.activation(
-                out=u_grouped[:, b * PAIR : (b + 1) * PAIR, :].rearrange("p o (u e) -> p o u e", u=2),
-                in_=u_turned[:].bitcast(BF16).rearrange("p u (o e) -> p o u e", e=2),
-                func=SIGN,
+                out=pairs, in_=u_turned[:].bitcast(BF16).rearrange("p w (q e) -> p q w e", e=2), func=SIGN
             )
 
         def pack_u(chunk, u_grouped):
@@ -128,8 +150,8 @@ def tile_binaryfactoredlinear_pa_kernel(tc, x, U_latent, V_latent, s1, s2, bias,
                 in_=u_grouped[:].rearrange("p o j -> p (o j)"),
             )
 
-        def turn_and_scale_x(x_piece, g, a_piece):
-            x_turned = psum.tile([P, 2, 2, P], F32, tag="turned")
+        def turn_and_scale_x(x_piece, g, a_piece, role):
+            x_turned = bank([P, 2, 2, P], F32, role)
             for u in range(2):
                 for n in range(2):
                     first_word = (2 * n + u) * P
@@ -210,7 +232,7 @@ def tile_binaryfactoredlinear_pa_kernel(tc, x, U_latent, V_latent, s1, s2, bias,
             v_raws.append(v_raw)
             x_raws.append(x_raw)
 
-        s2_turned = psum.tile([P, 2, 2, P], F32, tag="turned")
+        s2_turned = bank([P, 2, 2, P], F32, "first x")
         nc.tensor.transpose(s2_turned[:, 0, 0, :], s2_rows[:].bitcast(F32), identity[:])
         s2_words = consts.tile([P, 2 * PASSES], F32)
         nc.vector.tensor_copy(out=s2_words[:], in_=s2_turned[:, 0, 0, 0 : 2 * PASSES])
@@ -218,8 +240,7 @@ def tile_binaryfactoredlinear_pa_kernel(tc, x, U_latent, V_latent, s1, s2, bias,
 
         h_open = []
         for j in range(PACK):
-            tag = "h" if j == PACK - 1 else "sums"
-            h_bank = psum.tile([P, HALF], F32, tag=tag, bufs=1 if j == PACK - 1 else 3, name="h_bank")
+            h_bank = bank([P, HALF], F32, "first h")
             h_open.append((j, h_bank))
         u_raws = []
         odd_v = None
@@ -231,7 +252,7 @@ def tile_binaryfactoredlinear_pa_kernel(tc, x, U_latent, V_latent, s1, s2, bias,
             odd_v = sign_v(v_raws[s], V_PER_SLICE * s + 1)
             a_grouped = pool.tile([P, V_PER_SLICE, HALF, PACK], BF16, tag="a_grouped", align_bytes=64)
             for n in range(TILES_PER_HALF):
-                turn_and_scale_x(x_raws[s][:, n, :], V_PER_SLICE * s, a_grouped[:, :, n * P : (n + 1) * P, :])
+                turn_and_scale_x(x_raws[s][:, n, :], V_PER_SLICE * s, a_grouped[:, :, n * P : (n + 1) * P, :], "first x")
                 if s > 0 and n % 2 == 1:
                     first_matmul_pass(V_PER_SLICE * (s - 1) + n // 2, a_packed, h_open)
             pack_v(V_PER_SLICE * s, even_v)
@@ -244,25 +265,25 @@ def tile_binaryfactoredlinear_pa_kernel(tc, x, U_latent, V_latent, s1, s2, bias,
                         out=gain_rows_bf16[row * CHANNEL_TILES : (row + 1) * CHANNEL_TILES, :],
                         in_=vector.rearrange("(c p) -> c p", p=P),
                     )
-            direct_channels = slice(s * U_CHUNK + BLOCK, (s + 1) * U_CHUNK)
-            nc.sync.dma_start(out=s1_spread[:, s, :], in_=s1[direct_channels].partition_broadcast(P))
-            nc.sync.dma_start(out=bias_spread[:, s, :], in_=bias[direct_channels].partition_broadcast(P))
+            if s % 2 == 1:
+                for chunk in range(s - 1, s + 1):
+                    channels = slice((chunk + 1) * U_CHUNK - DIRECT, (chunk + 1) * U_CHUNK)
+                    nc.sync.dma_start(out=s1_spread[:, chunk, :], in_=s1[channels].partition_broadcast(P))
+                    nc.sync.dma_start(out=bias_spread[:, chunk, :], in_=bias[channels].partition_broadcast(P))
         pack_v(PASSES - 1, odd_v)
 
         def turn_gains():
             gain_rows = consts.tile([P, P], F32)
             nc.vector.tensor_copy(out=gain_rows[:], in_=gain_rows_bf16[:])
-            gain_turned = psum.tile([P, 2, 2, P], F32, tag="turned")
+            gain_turned = bank([P, 2, 2, P], F32, "x")
             nc.tensor.transpose(gain_turned[:, 0, 0, :], gain_rows[:], identity[:])
             nc.vector.tensor_copy(out=gain_cols[:], in_=gain_turned[:, 0, 0, 0 : 2 * CHANNEL_TILES])
 
-        def start_turned(half, i):
-            chunk, tile = divmod(i, STEPS)
-            c = chunk * (U_CHUNK // P) + tile
+        def start_turned(half, c, on_vector):
             tokens = slice(half * HALF, (half + 1) * HALF)
             gain = gain_cols[:, c : c + 1]
             offset = gain_cols[:, CHANNEL_TILES + c : CHANNEL_TILES + c + 1]
-            z_sums = psum.tile([P, HALF], F32, tag="sums", bufs=3)
+            z_sums = bank([P, HALF], F32, "late z" if half == 1 else "z")
             nc.tensor.matmul_mx(
                 out=z_sums[:],
                 lhsT=u_words[:, c * P : (c + 1) * P].bitcast(FP8X4),
@@ -272,128 +293,156 @@ def tile_binaryfactoredlinear_pa_kernel(tc, x, U_latent, V_latent, s1, s2, bias,
                 start=True,
                 stop=True,
             )
-            z_tile = pool.tile([P, HALF], F32, tag="z_tile", bufs=7)
-            if tile % 2 == 0:
+            z_tile = pool.tile([P, HALF], F32, tag="z_tile", bufs=8)
+            if on_vector:
                 nc.vector.tensor_scalar(out=z_tile[:], in0=z_sums[:], scalar1=gain, scalar2=offset, op0=MULT, op1=ADD)
             else:
                 nc.scalar.activation(out=z_tile[:], in_=z_sums[:], func=IDENTITY, scale=gain, bias=offset)
             return z_tile
 
-        def turn_back(z_pair, a, first_col, result):
-            z_back = psum.tile([P, 2, PAIR], F32, tag="turned")
+        def turn_back(z_pair, a, first_col, result, role):
+            z_back = bank([P, 2, PAIR], F32, role)
             for n in range(2):
                 tokens = slice((2 * a + n) * P, (2 * a + n + 1) * P)
                 for j in range(2):
                     nc.tensor.transpose(z_back[:, n, j * P : (j + 1) * P], z_pair[j][:, tokens], identity[:])
-            nc.scalar.copy(out=result[:, 2 * a : 2 * a + 2, first_col : first_col + PAIR], in_=z_back[:])
+            nc.scalar.copy(out=result[:, :, first_col : first_col + PAIR], in_=z_back[:])
 
-        def direct(half, i, result):
-            chunk, tile = divmod(i, STEPS)
-            u_cols = slice(chunk * U_CHUNK + BLOCK, (chunk + 1) * U_CHUNK)
+        def direct(half, chunk, tile, result):
+            first = TURNED[half]
+            width = U_CHUNK - first
             tokens = slice((half * TILES_PER_HALF + tile) * P, (half * TILES_PER_HALF + tile + 1) * P)
-            z_direct = psum.tile([P, BLOCK], F32, tag="sums", bufs=3)
-            nc.tensor.matmul_mx(
-                out=z_direct[:],
-                lhsT=h_words[:, tokens].bitcast(FP8X4),
-                lhsT_scale=h_scales[:, tokens],
-                rhs=u_words[:, u_cols].bitcast(FP8X4),
-                rhs_scale=u_scales[:, u_cols],
-                start=True,
-                stop=True,
+            z_gained = pool.tile([P, DIRECT], F32, tag="z_gained", bufs=3)
+            for start in range(0, width, BANK):
+                columns = min(BANK, width - start)
+                u_cols = slice(chunk * U_CHUNK + first + start, chunk * U_CHUNK + first + start + columns)
+                spread_cols = slice(first - min(TURNED) + start, first - min(TURNED) + start + columns)
+                z_direct = bank([P, columns], F32, "late d" if half == 1 else "d")
+                nc.tensor.matmul_mx(
+                    out=z_direct[:],
+                    lhsT=h_words[:, tokens].bitcast(FP8X4),
+                    lhsT_scale=h_scales[:, tokens],
+                    rhs=u_words[:, u_cols].bitcast(FP8X4),
+                    rhs_scale=u_scales[:, u_cols],
+                    start=True,
+                    stop=True,
+                )
+                nc.vector.tensor_tensor(
+                    out=z_gained[:, start : start + columns],
+                    in0=z_direct[:],
+                    in1=s1_spread[:, chunk, spread_cols],
+                    op=MULT,
+                )
+            nc.gpsimd.tensor_tensor(
+                out=result[:, tile % 2, first:U_CHUNK],
+                in0=z_gained[:, 0:width],
+                in1=bias_spread[:, chunk, first - min(TURNED) : DIRECT],
+                op=ADD,
             )
-            z_gained = pool.tile([P, BLOCK], F32, tag="z_gained", bufs=4)
-            nc.vector.tensor_tensor(out=z_gained[:], in0=z_direct[:], in1=s1_spread[:, chunk, :], op=MULT)
-            nc.gpsimd.tensor_tensor(out=result[:, tile, :], in0=z_gained[:], in1=bias_spread[:, chunk, :], op=ADD)
 
         pieces = SLICES * STEPS
-        GROUP_LAG = STEPS + 2
-        LAG = 7
+        GROUP_LAG = 5
+        LAG = 2
         BACK_LAG = 4
-        u_grouped = None
-        a_grouped = None
-        u_waiting = None
-        h_raw = None
-        h_sums = None
-        h_grouped = None
+
+        def spread_over_steps(step, count):
+            return range(step * count // STEPS, (step + 1) * count // STEPS)
+
+        def turn_u(n):
+            chunk, b = divmod(n, STEPS)
+            if b == 0:
+                u_tiles[chunk] = pool.tile([P, U_CHUNK, PACK], BF16, tag="u_grouped", align_bytes=64, name="u_tile")
+            turn_and_sign_u(u_raws[chunk], b, u_tiles[chunk], "first u" if chunk == 0 else "u")
+
+        def turn_x(n):
+            tile, b = divmod(n, STEPS)
+            if b == 0:
+                a_tiles[tile] = pool.tile([P, PASSES, P, PACK], BF16, tag="a_grouped", align_bytes=64, name="a_tile")
+            turn_and_scale_x(
+                x_raws[SLICES + tile][:, b * X_COLS : (b + 1) * X_COLS], 2 * b, a_tiles[tile][:, 2 * b : 2 * b + 2, :, :], "x"
+            )
+
+        def finish_piece(m, late):
+            half, i = divmod(m, pieces)
+            chunk, step = divmod(i, STEPS)
+            units = TURNED[half] // PAIR
+            for n in spread_over_steps(step, 2 * units):
+                unit, a = divmod(n, 2)
+                z_pair = (z_tiles[half, chunk, 2 * unit], z_tiles[half, chunk, 2 * unit + 1])
+                turn_back(z_pair, a, unit * PAIR, results[half, chunk, a], "late back" if late else "back")
+                if unit == units - 1:
+                    first_tile = half * TILES_PER_HALF + 2 * a
+                    nc.sync.dma_start(
+                        out=out_view[:, first_tile : first_tile + 2, chunk * U_CHUNK : (chunk + 1) * U_CHUNK],
+                        in_=results[half, chunk, a][:],
+                    )
+
+        def start_piece(m):
+            half, i = divmod(m, pieces)
+            chunk, step = divmod(i, STEPS)
+            for t in spread_over_steps(step, TURNED[half] // P):
+                z_tiles[half, chunk, t] = start_turned(half, chunk * (U_CHUNK // P) + t, t % 2 == 0)
+            if step % 2 == 0:
+                results[half, chunk, step // 2] = big_tile([P, 2, U_CHUNK], F32)
+            direct(half, chunk, step, results[half, chunk, step // 2])
+
+        def multiply(group):
+            tile, j = divmod(group, PACK)
+            if j == 0:
+                h_tiles[tile] = bank([P, PACK, P], F32, "h")
+            first_matmul_group(j, second_packed[tile], h_tiles[tile])
+
+        def quantising(k):
+            group = k - GROUP_LAG
+            if k % STEPS == STEPS - 1 and k < pieces:
+                second_packed.append(pack_a(a_tiles[k // STEPS], PASSES, P))
+            if k % STEPS == 0 and k < pieces:
+                pack_u(k // STEPS, u_tiles[k // STEPS])
+            if 0 < group <= pieces and group % PACK == 0:
+                pack_tile(TILES_PER_HALF + group // PACK - 1, h_grouped[group // PACK - 1])
+            if 0 <= group < pieces and group % PACK == PACK - 1:
+                tile = group // PACK
+                h_grouped[tile] = pool.tile([P, P, PACK], BF16, tag="h_grouped", align_bytes=64, name="h_tile")
+                nc.scalar.copy(out=h_grouped[tile][:], in_=h_tiles[tile][:].rearrange("p j t -> p t j"))
+
+        a_tiles = {}
+        u_tiles = {}
+        h_tiles = {}
+        h_grouped = {}
         second_packed = []
         z_tiles = {}
-        result_turned = None
-        result_direct = None
-        for k in range(LAG + 2 * pieces + BACK_LAG):
-            s, b = divmod(k, STEPS)
-            m = k - LAG
-            group = k - GROUP_LAG
-            if k < pieces:
-                if b == 0:
-                    a_ready = a_grouped
-                    u_waiting = u_grouped
-                    a_grouped = pool.tile([P, PASSES, P, PACK], BF16, tag="a_grouped", align_bytes=64)
-                    u_grouped = pool.tile([P, U_CHUNK, PACK], BF16, tag="u_grouped", align_bytes=64)
-                turn_and_sign_u(u_raws[s], b, u_grouped)
-                turn_and_scale_x(
-                    x_raws[SLICES + s][:, b * X_COLS : (b + 1) * X_COLS], 2 * b, a_grouped[:, 2 * b : 2 * b + 2, :, :]
-                )
-            elif k == pieces:
-                a_ready = a_grouped
-                u_waiting = u_grouped
-            back = m - BACK_LAG
-            if back >= 0:
-                half, i = divmod(back, pieces)
-                chunk, rest = divmod(i, STEPS)
-                unit, a = divmod(rest, 2)
-                if rest == 0:
-                    result_turned = big_tile([P, TILES_PER_HALF, BLOCK], F32)
-                turn_back((z_tiles[back - a], z_tiles[back - a + 1]), a, unit * PAIR, result_turned)
-                if a == 1:
-                    columns = slice(unit * PAIR, (unit + 1) * PAIR)
-                    channels = slice(chunk * U_CHUNK + unit * PAIR, chunk * U_CHUNK + (unit + 1) * PAIR)
-                    nc.sync.dma_start(
-                        out=out_view[:, half * TILES_PER_HALF : (half + 1) * TILES_PER_HALF, channels],
-                        in_=result_turned[:, :, columns],
-                    )
-            if k == STEPS - 1:
-                turn_gains()
-            if k < PACK:
-                first_matmul_pass(PASSES - V_PER_SLICE + k // 2, a_packed, h_open[2 * (k % 2) : 2 * (k % 2) + 2])
-            if 0 <= group < pieces:
-                j = group % PACK
-                if j == 0:
-                    h_sums = psum.tile([P, PACK, P], F32, tag="h", bufs=1)
-                first_matmul_group(j, second_packed[group // PACK], h_sums)
-            if 0 <= m < 2 * pieces:
-                half, i = divmod(m, pieces)
-                chunk, tile = divmod(i, STEPS)
-                z_tiles[m] = start_turned(half, i)
-                if tile == 0:
-                    result_direct = big_tile([P, TILES_PER_HALF, BLOCK], F32)
-                direct(half, i, result_direct)
-                if tile % 2 == 1:
-                    first_channel = chunk * U_CHUNK + BLOCK
-                    first_tile = half * TILES_PER_HALF + tile - 1
-                    nc.sync.dma_start(
-                        out=out_view[:, first_tile : first_tile + 2, first_channel : first_channel + BLOCK],
-                        in_=result_direct[:, tile - 1 : tile + 1, :],
-                    )
-            if k == PACK:
-                h_raw = pool.tile([P, PACK, HALF], BF16, tag="h_raw", bufs=1)
-                for j, h_bank in h_open:
-                    nc.scalar.copy(out=h_raw[:, j, :], in_=h_bank[:])
-            if k == PACK + 1:
-                h_grouped = pool.tile([P, HALF, PACK], BF16, tag="h_grouped", align_bytes=64)
-                nc.vector.tensor_copy(out=h_grouped[:], in_=h_raw[:].rearrange("p j t -> p t j"))
-            if k == PACK + 2:
-                nc.vector.quantize_mx(
-                    out=h_words[:, 0:HALF].bitcast(FP8X4),
-                    scales=h_scales[:, 0:HALF],
-                    in_=h_grouped[:].rearrange("p t j -> p (t j)"),
-                )
-            if 0 < s <= SLICES:
-                if b == 0:
-                    second_packed.append(pack_a(a_ready, PASSES, P))
-                elif b == 1:
-                    pack_u(s - 1, u_waiting)
-            if 0 < group <= pieces and group % PACK == 0:
-                pack_tile(TILES_PER_HALF + group // PACK - 1, h_grouped)
-            if 0 <= group < pieces and group % PACK == PACK - 1:
-                h_grouped = pool.tile([P, P, PACK], BF16, tag="h_grouped", align_bytes=64)
-                nc.scalar.copy(out=h_grouped[:], in_=h_sums[:].rearrange("p j t -> p t j"))
+        results = {}
+
+        for n in range(STEPS):
+            turn_u(n)
+        for g in range(PASSES - V_PER_SLICE, PASSES):
+            first_matmul_pass(g, a_packed, h_open)
+        turn_gains()
+        h_raw = pool.tile([P, PACK, HALF], BF16, tag="h_raw", bufs=1)
+        h_first = pool.tile([P, HALF, PACK], BF16, tag="h_grouped", align_bytes=64)
+        for j, h_bank in h_open:
+            nc.vector.tensor_copy(out=h_raw[:, j, :], in_=h_bank[:])
+        nc.vector.tensor_copy(out=h_first[:], in_=h_raw[:].rearrange("p j t -> p t j"))
+        turn_x(0)
+        nc.vector.quantize_mx(
+            out=h_words[:, 0:HALF].bitcast(FP8X4),
+            scales=h_scales[:, 0:HALF],
+            in_=h_first[:].rearrange("p t j -> p (t j)"),
+        )
+        started = {}
+        for k in range(22 + pieces + BACK_LAG):
+            if k - BACK_LAG in started:
+                finish_piece(started[k - BACK_LAG], k >= 22)
+            if STEPS + k < pieces:
+                turn_u(STEPS + k)
+            if 0 < k < pieces:
+                turn_x(k)
+            if 0 <= k - GROUP_LAG < pieces:
+                multiply(k - GROUP_LAG)
+            if LAG <= k < LAG + pieces:
+                started[k] = k - LAG
+            elif 22 <= k < 22 + pieces:
+                started[k] = pieces + k - 22
+            if k in started:
+                start_piece(started[k])
+            quantising(k)

@@ -42,15 +42,8 @@ BANKS = {
     "first x": (0, 1, 2, 3),
     "first h": (4, 5, 6, 7),
     "first u": (0, 1, 2, 3),
-    "x": (0, 1),
-    "u": (2, 3),
-    "back": (4,),
-    "z": (5,),
-    "d": (6,),
     "h": (7,),
-    "late back": (0, 1, 2, 3),
-    "late z": (4, 5),
-    "late d": (6, 7),
+    "shared": (0, 1, 2, 3, 4, 5, 6),
 }
 
 FLOPS = 2 * TOKENS * D_IN * RANK + 2 * TOKENS * RANK * D_OUT
@@ -90,6 +83,7 @@ def tile_binaryfactoredlinear_pa_kernel(tc, x, U_latent, V_latent, s1, s2, bias,
         turn = {}
 
         def bank(shape, dtype, role):
+            role = role if role in BANKS else "shared"
             numbers = BANKS[role]
             turn[role] = turn.get(role, -1) + 1
             tile = psum.tile(shape, dtype, tag="bank%d" % numbers[turn[role] % len(numbers)], bufs=1, name="bank")
@@ -342,8 +336,8 @@ def tile_binaryfactoredlinear_pa_kernel(tc, x, U_latent, V_latent, s1, s2, bias,
 
         pieces = SLICES * STEPS
         GROUP_LAG = 5
-        LAG = 2
-        BACK_LAG = 4
+        LAG = 4
+        BACK_LAG = 3
 
         def spread_over_steps(step, count):
             return range(step * count // STEPS, (step + 1) * count // STEPS)
@@ -377,11 +371,15 @@ def tile_binaryfactoredlinear_pa_kernel(tc, x, U_latent, V_latent, s1, s2, bias,
                         in_=results[half, chunk, a][:],
                     )
 
-        def start_piece(m):
+        def start_piece_z(m):
             half, i = divmod(m, pieces)
             chunk, step = divmod(i, STEPS)
             for t in spread_over_steps(step, TURNED[half] // P):
                 z_tiles[half, chunk, t] = start_turned(half, chunk * (U_CHUNK // P) + t, t % 2 == 0)
+
+        def start_piece_d(m):
+            half, i = divmod(m, pieces)
+            chunk, step = divmod(i, STEPS)
             if step % 2 == 0:
                 results[half, chunk, step // 2] = big_tile([P, 2, U_CHUNK], F32)
             direct(half, chunk, step, results[half, chunk, step // 2])
@@ -396,7 +394,7 @@ def tile_binaryfactoredlinear_pa_kernel(tc, x, U_latent, V_latent, s1, s2, bias,
             group = k - GROUP_LAG
             if k % STEPS == STEPS - 1 and k < pieces:
                 second_packed.append(pack_a(a_tiles[k // STEPS], PASSES, P))
-            if k % STEPS == 0 and k < pieces:
+            if k % STEPS == 0 and 0 < k < pieces:
                 pack_u(k // STEPS, u_tiles[k // STEPS])
             if 0 < group <= pieces and group % PACK == 0:
                 pack_tile(TILES_PER_HALF + group // PACK - 1, h_grouped[group // PACK - 1])
@@ -421,28 +419,39 @@ def tile_binaryfactoredlinear_pa_kernel(tc, x, U_latent, V_latent, s1, s2, bias,
         h_raw = pool.tile([P, PACK, HALF], BF16, tag="h_raw", bufs=1)
         h_first = pool.tile([P, HALF, PACK], BF16, tag="h_grouped", align_bytes=64)
         for j, h_bank in h_open:
-            nc.vector.tensor_copy(out=h_raw[:, j, :], in_=h_bank[:])
-        nc.vector.tensor_copy(out=h_first[:], in_=h_raw[:].rearrange("p j t -> p t j"))
+            if j >= 1:
+                nc.scalar.copy(out=h_raw[:, j, :], in_=h_bank[:])
+            else:
+                nc.vector.tensor_copy(out=h_raw[:, j, :], in_=h_bank[:])
         turn_x(0)
+        pack_u(0, u_tiles[0])
+        nc.vector.tensor_copy(out=h_first[:], in_=h_raw[:].rearrange("p j t -> p t j"))
+        turn_x(1)
         nc.vector.quantize_mx(
             out=h_words[:, 0:HALF].bitcast(FP8X4),
             scales=h_scales[:, 0:HALF],
             in_=h_first[:].rearrange("p t j -> p (t j)"),
         )
         started = {}
-        for k in range(22 + pieces + BACK_LAG):
-            if k - BACK_LAG in started:
-                finish_piece(started[k - BACK_LAG], k >= 22)
-            if STEPS + k < pieces:
-                turn_u(STEPS + k)
-            if 0 < k < pieces:
-                turn_x(k)
-            if 0 <= k - GROUP_LAG < pieces:
-                multiply(k - GROUP_LAG)
-            if LAG <= k < LAG + pieces:
-                started[k] = k - LAG
-            elif 22 <= k < 22 + pieces:
-                started[k] = pieces + k - 22
-            if k in started:
-                start_piece(started[k])
-            quantising(k)
+        last_step = 22 + pieces + BACK_LAG
+        for first_step in range(0, last_step, 1):
+            steps = range(first_step, first_step + 1)
+            for k in steps:
+                if LAG <= k < LAG + pieces:
+                    started[k] = k - LAG
+                elif 22 <= k < 22 + pieces:
+                    started[k] = pieces + k - 22
+                if STEPS + k < pieces:
+                    turn_u(STEPS + k)
+                if 1 < k < pieces:
+                    turn_x(k)
+                if k - BACK_LAG in started:
+                    finish_piece(started[k - BACK_LAG], k >= 22)
+            for k in steps:
+                if 0 <= k - GROUP_LAG < pieces:
+                    multiply(k - GROUP_LAG)
+                if k in started:
+                    start_piece_z(started[k])
+                if k in started:
+                    start_piece_d(started[k])
+                quantising(k)

@@ -247,8 +247,9 @@ def tile_binaryfactoredlinear_pa_kernel(tc, x, U_latent, V_latent, s1, s2, bias,
             a_grouped = pool.tile([P, V_PER_SLICE, HALF, PACK], BF16, tag="a_grouped", align_bytes=64)
             for n in range(TILES_PER_HALF):
                 turn_and_scale_x(x_raws[s][:, n, :], V_PER_SLICE * s, a_grouped[:, :, n * P : (n + 1) * P, :], "first x")
-                if s > 0 and n % 2 == 1:
-                    first_matmul_pass(V_PER_SLICE * (s - 1) + n // 2, a_packed, h_open)
+                if s > 0 and n == 3:
+                    for g in range(V_PER_SLICE * (s - 1), V_PER_SLICE * s):
+                        first_matmul_pass(g, a_packed, h_open)
             pack_v(V_PER_SLICE * s, even_v)
             a_packed = pack_a(a_grouped, V_PER_SLICE, HALF)
             u_raws.append(load_u(s))
@@ -337,7 +338,7 @@ def tile_binaryfactoredlinear_pa_kernel(tc, x, U_latent, V_latent, s1, s2, bias,
         pieces = SLICES * STEPS
         GROUP_LAG = 5
         LAG = 4
-        BACK_LAG = 3
+        BACK_LAG = 4
 
         def spread_over_steps(step, count):
             return range(step * count // STEPS, (step + 1) * count // STEPS)
@@ -434,24 +435,25 @@ def tile_binaryfactoredlinear_pa_kernel(tc, x, U_latent, V_latent, s1, s2, bias,
         )
         started = {}
         last_step = 22 + pieces + BACK_LAG
-        for first_step in range(0, last_step, 1):
-            steps = range(first_step, first_step + 1)
-            for k in steps:
-                if LAG <= k < LAG + pieces:
-                    started[k] = k - LAG
-                elif 22 <= k < 22 + pieces:
-                    started[k] = pieces + k - 22
-                if STEPS + k < pieces:
-                    turn_u(STEPS + k)
-                if 1 < k < pieces:
-                    turn_x(k)
-                if k - BACK_LAG in started:
-                    finish_piece(started[k - BACK_LAG], k >= 22)
-            for k in steps:
-                if 0 <= k - GROUP_LAG < pieces:
-                    multiply(k - GROUP_LAG)
-                if k in started:
-                    start_piece_z(started[k])
-                if k in started:
-                    start_piece_d(started[k])
-                quantising(k)
+        k = 0
+        while k < last_step:
+            steps = range(k, min(k + (2 if k >= 16 else 1), last_step))
+            k = steps.stop
+            for n in steps:
+                if LAG <= n < LAG + pieces:
+                    started[n] = n - LAG
+                elif 22 <= n < 22 + pieces:
+                    started[n] = pieces + n - 22
+                if STEPS + n < pieces:
+                    turn_u(STEPS + n)
+                if 1 < n < pieces:
+                    turn_x(n)
+                if n - BACK_LAG in started:
+                    finish_piece(started[n - BACK_LAG], n >= 22)
+            for n in steps:
+                if 0 <= n - GROUP_LAG < pieces:
+                    multiply(n - GROUP_LAG)
+                if n in started:
+                    start_piece_z(started[n])
+                    start_piece_d(started[n])
+                quantising(n)

@@ -108,11 +108,13 @@ def tile_binaryfactoredlinear_pa_kernel(tc, x, U_latent, V_latent, s1, s2, bias,
             v_grouped = pool.tile([P, RANK, PACK], BF16, tag="v_grouped", bufs=3, align_bytes=64)
             for u in range(2):
                 cols = slice(u * PAIR, (u + 1) * PAIR)
-                nc.scalar.activation(
-                    out=v_grouped[:, cols, :].rearrange("p (e q) j -> p q j e", e=2),
-                    in_=v_raw[:, g % V_PER_SLICE, :, cols].rearrange("p j (q e) -> p q j e", e=2),
-                    func=SIGN,
-                )
+                for e in range(2):
+                    block = slice((2 * u + e) * P, (2 * u + e + 1) * P)
+                    nc.scalar.activation(
+                        out=v_grouped[:, block, :],
+                        in_=v_raw[:, g % V_PER_SLICE, :, cols].rearrange("p j (q e) -> p e q j", e=2)[:, e],
+                        func=SIGN,
+                    )
             return v_grouped
 
         def pack_v(g, v_grouped):

@@ -73,8 +73,11 @@ def tile_binaryfactoredlinear_pa_kernel(tc, x, U_latent, V_latent, s1, s2, bias,
         h_words = consts.tile([P, TOKENS], U32, align_bytes=64)
         h_scales = consts.tile([P, TOKENS], U8, align_bytes=64)
         gain_cols = consts.tile([P, 2 * CHANNEL_TILES], F32)
-        s1_spread = consts.tile([P, SLICES, DIRECT], BF16)
-        bias_spread = consts.tile([P, SLICES, DIRECT], BF16)
+        spread = consts.tile([P, SLICES, 2, DIRECT], BF16)
+        direct_rows = consts.tile([P, 2, DIRECT], BF16)
+        nc.gpsimd.memset(direct_rows[:].rearrange("p v c -> p (v c)").bitcast(F32), 0.0)
+        ones = consts.tile([P, P], BF16)
+        nc.gpsimd.memset(ones[:], 1.0)
 
         def big_tile(shape, dtype):
             tile = pool.tile(shape, dtype, tag="big", bufs=10, name="big")
@@ -262,12 +265,21 @@ def tile_binaryfactoredlinear_pa_kernel(tc, x, U_latent, V_latent, s1, s2, bias,
                         out=gain_rows_bf16[row * CHANNEL_TILES : (row + 1) * CHANNEL_TILES, :],
                         in_=vector.rearrange("(c p) -> c p", p=P),
                     )
-            if s % 2 == 1:
-                for chunk in range(s - 1, s + 1):
-                    channels = slice((chunk + 1) * U_CHUNK - DIRECT, (chunk + 1) * U_CHUNK)
-                    nc.sync.dma_start(out=s1_spread[:, chunk, :], in_=s1[channels].partition_broadcast(P))
-                    nc.sync.dma_start(out=bias_spread[:, chunk, :], in_=bias[channels].partition_broadcast(P))
+                for row, vector in enumerate((s1, bias)):
+                    nc.sync.dma_start(
+                        out=direct_rows[0:1, row, :], in_=vector[U_CHUNK - DIRECT : U_CHUNK].rearrange("(o c) -> o c", o=1)
+                    )
+        for chunk in range(1, SLICES):
+            channels = slice((chunk + 1) * U_CHUNK - DIRECT, (chunk + 1) * U_CHUNK)
+            for row, vector in enumerate((s1, bias)):
+                nc.sync.dma_start(out=spread[:, chunk, row, :], in_=vector[channels].partition_broadcast(P))
         pack_v(PASSES - 1, odd_v)
+
+        def spread_first_rows():
+            rows = bank([P, 2, DIRECT], BF16, "x")
+            for row in range(2):
+                nc.tensor.matmul(rows[:, row, :], lhsT=ones[:], rhs=direct_rows[:, row, :], start=True, stop=True)
+            nc.scalar.copy(out=spread[:, 0], in_=rows[:])
 
         def turn_gains():
             gain_rows = consts.tile([P, P], F32)
@@ -327,13 +339,13 @@ def tile_binaryfactoredlinear_pa_kernel(tc, x, U_latent, V_latent, s1, s2, bias,
                 nc.vector.tensor_tensor(
                     out=z_gained[:, start : start + columns],
                     in0=z_direct[:],
-                    in1=s1_spread[:, chunk, spread_cols],
+                    in1=spread[:, chunk, 0, spread_cols],
                     op=MULT,
                 )
             nc.gpsimd.tensor_tensor(
                 out=result[:, tile % 2, first:U_CHUNK],
                 in0=z_gained[:, 0:width],
-                in1=bias_spread[:, chunk, first - min(TURNED) : DIRECT],
+                in1=spread[:, chunk, 1, first - min(TURNED) : DIRECT],
                 op=ADD,
             )
 
@@ -419,6 +431,7 @@ def tile_binaryfactoredlinear_pa_kernel(tc, x, U_latent, V_latent, s1, s2, bias,
         for g in range(PASSES - V_PER_SLICE, PASSES):
             first_matmul_pass(g, a_packed, h_open)
         turn_gains()
+        spread_first_rows()
         h_raw = pool.tile([P, PACK, HALF], BF16, tag="h_raw", bufs=1)
         h_first = pool.tile([P, HALF, PACK], BF16, tag="h_grouped", align_bytes=64)
         for j, h_bank in h_open:

@@ -321,7 +321,7 @@ def tile_binaryfactoredlinear_pa_kernel(tc, x, U_latent, V_latent, s1, s2, bias,
             first = TURNED[half]
             width = U_CHUNK - first
             tokens = slice((half * TILES_PER_HALF + tile) * P, (half * TILES_PER_HALF + tile + 1) * P)
-            z_gained = pool.tile([P, DIRECT], F32, tag="z_gained", bufs=3)
+            z_gained = pool.tile([P, DIRECT], F32, tag="z_gained", bufs=4)
             for start in range(0, width, BANK):
                 columns = min(BANK, width - start)
                 u_cols = slice(chunk * U_CHUNK + first + start, chunk * U_CHUNK + first + start + columns)
@@ -390,7 +390,7 @@ def tile_binaryfactoredlinear_pa_kernel(tc, x, U_latent, V_latent, s1, s2, bias,
             half, i = divmod(m, pieces)
             chunk, step = divmod(i, STEPS)
             for t in spread_over_steps(step, TURNED[half] // P):
-                z_tiles[half, chunk, t] = start_turned(half, chunk * (U_CHUNK // P) + t, t % 2 == 0)
+                z_tiles[half, chunk, t] = start_turned(half, chunk * (U_CHUNK // P) + t, (t % 2 == 0) if half == 1 else (t in (1, 2)))
 
         def start_piece_d(m):
             half, i = divmod(m, pieces)
@@ -461,14 +461,15 @@ def tile_binaryfactoredlinear_pa_kernel(tc, x, U_latent, V_latent, s1, s2, bias,
                     started[n] = pieces + n - 22
                 if STEPS + n < pieces:
                     turn_u(STEPS + n)
-                if 1 < n < pieces:
-                    turn_x(n)
                 if n - BACK_LAG in started:
                     finish_piece(started[n - BACK_LAG], n >= 22)
+                if 1 < n < pieces:
+                    turn_x(n)
             for n in steps:
-                if 0 <= n - GROUP_LAG < pieces:
-                    multiply(n - GROUP_LAG)
                 if n in started:
                     start_piece_z(started[n])
+                if n in started:
                     start_piece_d(started[n])
+                if 0 <= n - GROUP_LAG < pieces:
+                    multiply(n - GROUP_LAG)
                 quantising(n)

@@ -390,7 +390,7 @@ def tile_binaryfactoredlinear_pa_kernel(tc, x, U_latent, V_latent, s1, s2, bias,
             half, i = divmod(m, pieces)
             chunk, step = divmod(i, STEPS)
             for t in spread_over_steps(step, TURNED[half] // P):
-                z_tiles[half, chunk, t] = start_turned(half, chunk * (U_CHUNK // P) + t, (t % 2 == 0) if half == 1 else (t in (1, 2)))
+                z_tiles[half, chunk, t] = start_turned(half, chunk * (U_CHUNK // P) + t, half == 1 and t % 2 == 0)
 
         def start_piece_d(m):
             half, i = divmod(m, pieces)

@@ -435,7 +435,7 @@ def tile_binaryfactoredlinear_pa_kernel(tc, x, U_latent, V_latent, s1, s2, bias,
         h_raw = pool.tile([P, PACK, HALF], BF16, tag="h_raw", bufs=1)
         h_first = pool.tile([P, HALF, PACK], BF16, tag="h_grouped", align_bytes=64)
         for j, h_bank in h_open:
-            if j >= 1:
+            if j >= 2:
                 nc.scalar.copy(out=h_raw[:, j, :], in_=h_bank[:])
             else:
                 nc.vector.tensor_copy(out=h_raw[:, j, :], in_=h_bank[:])
@@ -467,9 +467,9 @@ def tile_binaryfactoredlinear_pa_kernel(tc, x, U_latent, V_latent, s1, s2, bias,
                     turn_x(n)
             for n in steps:
                 if n in started:
-                    start_piece_z(started[n])
-                if n in started:
                     start_piece_d(started[n])
+                if n in started:
+                    start_piece_z(started[n])
                 if 0 <= n - GROUP_LAG < pieces:
                     multiply(n - GROUP_LAG)
                 quantising(n)

from contextlib import ExitStack

import concourse.masks as masks
import concourse.mybir as mybir

F32 = mybir.dt.float32
BF16 = mybir.dt.bfloat16
U32 = mybir.dt.uint32
U8 = mybir.dt.uint8
FP8X4 = mybir.dt.float8_e4m3fn_x4
SIGN = mybir.ActivationFunctionType.Sign
IDENTITY = mybir.ActivationFunctionType.Identity
MULT = mybir.AluOpType.mult
ADD = mybir.AluOpType.add

P = 128
PACK = 4
K_PASS = P * PACK
BANK = 512

TOKENS = 1024
D_IN = 4096
D_OUT = 4096
RANK = 512

PASSES = D_IN // K_PASS
TOKEN_TILES = TOKENS // P
HALF = BANK
TILES_PER_HALF = HALF // P
SLICES = 4
V_PER_SLICE = PASSES // SLICES
X_COLS = V_PER_SLICE * K_PASS
U_CHUNK = D_OUT // SLICES
PAIR = 2 * P

CHANNEL_TILES = D_OUT // P
STEPS = U_CHUNK // PAIR
TURNED = (2 * PAIR, 2 * PAIR)
DIRECT = U_CHUNK - min(TURNED)

BANKS = {
    "first x": (0, 1, 2, 3),
    "first h": (4, 5, 6, 7),
    "first u": (0, 1, 2, 3),
    "h": (7,),
    "shared": (0, 1, 2, 3, 4, 5, 6),
}

FLOPS = 2 * TOKENS * D_IN * RANK + 2 * TOKENS * RANK * D_OUT


def tile_binaryfactoredlinear_pa_kernel(tc, x, U_latent, V_latent, s1, s2, bias, out):
    nc = tc.nc
    x_rows = x.flatten_outer_dims()
    x_first = x_rows[0:HALF, :].rearrange("(n p) k -> p n k", p=P)
    v_view = V_latent.rearrange("(g u p e) r -> p g u (e r)", g=PASSES, u=2, p=P, e=2)
    u_view = U_latent.rearrange("(c p t) r -> p c (t r)", c=SLICES, p=P)
    out_view = out.flatten_outer_dims().rearrange("(n p) o -> p n o", p=P)

    with ExitStack() as stack:
        stack.enter_context(tc.manual_schedule())
        consts = stack.enter_context(tc.tile_pool(name="consts", bufs=1))
        pool = stack.enter_context(tc.tile_pool(name="pool", bufs=2))
        psum = stack.enter_context(tc.psum_pool(name="psum", bufs=4))

        identity = consts.tile([P, P], F32)
        masks.make_identity(nc, identity[:])

        v_words = consts.tile([P, PASSES, RANK], U32, align_bytes=64)
        v_scales = consts.tile([P, PASSES, RANK], U8, align_bytes=64)
        u_words = consts.tile([P, D_OUT], U32, align_bytes=64)
        u_scales = consts.tile([P, D_OUT], U8, align_bytes=64)
        h_words = consts.tile([P, TOKENS], U32, align_bytes=64)
        h_scales = consts.tile([P, TOKENS], U8, align_bytes=64)
        gain_cols = consts.tile([P, 2 * CHANNEL_TILES], F32)
        spread = consts.tile([P, SLICES, 2, DIRECT], BF16)
        direct_rows = consts.tile([P, 2, DIRECT], BF16)
        nc.gpsimd.memset(direct_rows[:].rearrange("p v c -> p (v c)").bitcast(F32), 0.0)
        ones = consts.tile([P, P], BF16)
        nc.gpsimd.memset(ones[:], 1.0)

        def big_tile(shape, dtype):
            tile = pool.tile(shape, dtype, tag="big", bufs=10, name="big")
            return tile

        turn = {}

        def bank(shape, dtype, role):
            role = role if role in BANKS else "shared"
            numbers = BANKS[role]
            turn[role] = turn.get(role, -1) + 1
            tile = psum.tile(shape, dtype, tag="bank%d" % numbers[turn[role] % len(numbers)], bufs=1, name="bank")
            return tile

        def load_v(v_raw, g):
            nc.sync.dma_start(
                out=v_raw[:, g % V_PER_SLICE].rearrange("p (u e) r -> p u (e r)", u=2), in_=v_view[:, g]
            )

        def load_u(chunk):
            u_raw = big_tile([P, U_CHUNK // P, RANK], BF16)
            nc.sync.dma_start(out=u_raw[:].rearrange("p t r -> p (t r)"), in_=u_view[:, chunk, :])
            return u_raw

        def load_x(i):
            x_raw = big_tile([P, D_IN], BF16)
            nc.sync.dma_start(out=x_raw[:], in_=x_rows[i * P : (i + 1) * P, :])
            return x_raw

        def sign_v(v_raw, g):
            v_grouped = pool.tile([P, RANK, PACK], BF16, tag="v_grouped", bufs=3, align_bytes=64)
            for u in range(2):
                cols = slice(u * PAIR, (u + 1) * PAIR)
                for e in range(2):
                    block = slice((2 * u + e) * P, (2 * u + e + 1) * P)
                    nc.scalar.activation(
                        out=v_grouped[:, block, :],
                        in_=v_raw[:, g % V_PER_SLICE, :, cols].rearrange("p j (q e) -> p e q j", e=2)[:, e],
                        func=SIGN,
                    )
            return v_grouped

        def pack_v(g, v_grouped):
            nc.vector.quantize_mx(
                out=v_words[:, g, :].bitcast(FP8X4),
                scales=v_scales[:, g, :],
                in_=v_grouped[:].rearrange("p c j -> p (c j)"),
            )

        def turn_and_sign_u(u_raw, b, u_grouped, role):
            u_turned = bank([P, 2 * 2, P], F32, role)
            for t in range(2):
                for u in range(2):
                    nc.tensor.transpose(
                        u_turned[:, 2 * t + u, :],
                        u_raw[:, 2 * b + t, :].bitcast(F32)[:, u * P : (u + 1) * P],
                        identity[:],
                    )
            pairs = u_grouped[:].rearrange("p (q t) (u e) -> p q (t u) e", q=P, u=2)[:, :, 4 * b : 4 * b + 4, :]
            nc.scalar.activation(
                out=pairs, in_=u_turned[:].bitcast(BF16).rearrange("p w (q e) -> p q w e", e=2), func=SIGN
            )

        def pack_u(chunk, u_grouped):
            cols = slice(chunk * U_CHUNK, (chunk + 1) * U_CHUNK)
            nc.vector.quantize_mx(
                out=u_words[:, cols].bitcast(FP8X4),
                scales=u_scales[:, cols],
                in_=u_grouped[:].rearrange("p o j -> p (o j)"),
            )

        def turn_and_scale_x(x_piece, g, a_piece, role):
            x_turned = bank([P, 2, 2, P], F32, role)
            for u in range(2):
                for n in range(2):
                    first_word = (2 * n + u) * P
                    nc.tensor.transpose(
                        x_turned[:, u, n, :], x_piece.bitcast(F32)[:, first_word : first_word + P], identity[:]
                    )
            gains = s2_values[:, g * PACK : (g + 2) * PACK]
            nc.vector.tensor_tensor(
                out=a_piece.rearrange("p g t (u e) -> p g t u e", u=2),
                in0=x_turned[:].bitcast(BF16).rearrange("p u g (t e) -> p g t u e", e=2),
                in1=gains.rearrange("p (g o u e) -> p g o u e", g=2, o=1, u=2).to_broadcast([P, 2, P, 2, 2]),
                op=MULT,
            )

        def pack_a(a_grouped, passes, tokens):
            a_words = pool.tile([P, passes, tokens], U32, tag="a_words", bufs=3, align_bytes=64)
            a_scales = pool.tile([P, passes, tokens], U8, tag="a_scales", bufs=3, align_bytes=64)
            nc.vector.quantize_mx(
                out=a_words[:].rearrange("p g t -> p (g t)").bitcast(FP8X4),
                scales=a_scales[:].rearrange("p g t -> p (g t)"),
                in_=a_grouped[:].rearrange("p g t j -> p (g t j)"),
            )
            return a_words, a_scales

        def first_matmul_pass(g, a_packed, h_banks):
            a_words, a_scales = a_packed
            n = g % V_PER_SLICE
            for j, h_bank in h_banks:
                cols = slice(j * P, (j + 1) * P)
                nc.tensor.matmul_mx(
                    out=h_bank[:],
                    lhsT=v_words[:, g, cols].bitcast(FP8X4),
                    lhsT_scale=v_scales[:, g, cols],
                    rhs=a_words[:, n, :].bitcast(FP8X4),
                    rhs_scale=a_scales[:, n, :],
                    start=(g == 0),
                    stop=(g == PASSES - 1),
                )

        def first_matmul_group(j, a_packed, h_sums):
            a_words, a_scales = a_packed
            cols = slice(j * P, (j + 1) * P)
            for g in range(PASSES):
                nc.tensor.matmul_mx(
                    out=h_sums[:, j, :],
                    lhsT=v_words[:, g, cols].bitcast(FP8X4),
                    lhsT_scale=v_scales[:, g, cols],
                    rhs=a_words[:, g, :].bitcast(FP8X4),
                    rhs_scale=a_scales[:, g, :],
                    start=(g == 0),
                    stop=(g == PASSES - 1),
                )

        def pack_tile(i, h_grouped):
            tokens = slice(i * P, (i + 1) * P)
            nc.vector.quantize_mx(
                out=h_words[:, tokens].bitcast(FP8X4),
                scales=h_scales[:, tokens],
                in_=h_grouped[:].rearrange("p t j -> p (t j)"),
            )

        s2_rows = consts.tile([P, PAIR], BF16)
        nc.vector.memset(s2_rows[:].bitcast(F32), 0.0)
        nc.sync.dma_start(out=s2_rows[0 : 2 * PASSES, :], in_=s2.rearrange("(a w) -> a w", w=PAIR))
        gain_rows_bf16 = consts.tile([P, P], BF16)
        nc.vector.memset(gain_rows_bf16[:].bitcast(F32), 0.0)

        v_raws = []
        x_raws = []
        for s in range(SLICES):
            v_raw = big_tile([P, V_PER_SLICE, PACK, RANK], BF16)
            x_raw = big_tile([P, TILES_PER_HALF, X_COLS], BF16)
            load_v(v_raw, V_PER_SLICE * s)
            for part in range(2):
                tiles = slice(2 * part, 2 * part + 2)
                nc.sync.dma_start(out=x_raw[:, tiles, :], in_=x_first[:, tiles, s * X_COLS : (s + 1) * X_COLS])
            load_v(v_raw, V_PER_SLICE * s + 1)
            v_raws.append(v_raw)
            x_raws.append(x_raw)

        s2_turned = bank([P, 2, 2, P], F32, "first x")
        nc.tensor.transpose(s2_turned[:, 0, 0, :], s2_rows[:].bitcast(F32), identity[:])
        s2_words = consts.tile([P, 2 * PASSES], F32)
        nc.vector.tensor_copy(out=s2_words[:], in_=s2_turned[:, 0, 0, 0 : 2 * PASSES])
        s2_values = s2_words[:].bitcast(BF16)

        h_open = []
        for j in range(PACK):
            h_bank = bank([P, HALF], F32, "first h")
            h_open.append((j, h_bank))
        u_raws = []
        odd_v = None
        a_packed = None
        for s in range(SLICES):
            if s > 0:
                pack_v(V_PER_SLICE * s - 1, odd_v)
            even_v = sign_v(v_raws[s], V_PER_SLICE * s)
            odd_v = sign_v(v_raws[s], V_PER_SLICE * s + 1)
            a_grouped = pool.tile([P, V_PER_SLICE, HALF, PACK], BF16, tag="a_grouped", align_bytes=64)
            for n in range(TILES_PER_HALF):
                turn_and_scale_x(x_raws[s][:, n, :], V_PER_SLICE * s, a_grouped[:, :, n * P : (n + 1) * P, :], "first x")
                if s > 0 and n == 3:
                    for g in range(V_PER_SLICE * (s - 1), V_PER_SLICE * s):
                        first_matmul_pass(g, a_packed, h_open)
            pack_v(V_PER_SLICE * s, even_v)
            a_packed = pack_a(a_grouped, V_PER_SLICE, HALF)
            u_raws.append(load_u(s))
            x_raws.append(load_x(TILES_PER_HALF + s))
            if s == 0:
                for row, vector in enumerate((s1, bias)):
                    nc.sync.dma_start(
                        out=gain_rows_bf16[row * CHANNEL_TILES : (row + 1) * CHANNEL_TILES, :],
                        in_=vector.rearrange("(c p) -> c p", p=P),
                    )
                for row, vector in enumerate((s1, bias)):
                    nc.sync.dma_start(
                        out=direct_rows[0:1, row, :], in_=vector[U_CHUNK - DIRECT : U_CHUNK].rearrange("(o c) -> o c", o=1)
                    )
        for chunk in range(1, SLICES):
            channels = slice((chunk + 1) * U_CHUNK - DIRECT, (chunk + 1) * U_CHUNK)
            for row, vector in enumerate((s1, bias)):
                nc.sync.dma_start(out=spread[:, chunk, row, :], in_=vector[channels].partition_broadcast(P))
        pack_v(PASSES - 1, odd_v)

        def spread_first_rows():
            rows = bank([P, 2, DIRECT], BF16, "x")
            for row in range(2):
                nc.tensor.matmul(rows[:, row, :], lhsT=ones[:], rhs=direct_rows[:, row, :], start=True, stop=True)
            nc.scalar.copy(out=spread[:, 0], in_=rows[:])

        def turn_gains():
            gain_rows = consts.tile([P, P], F32)
            nc.vector.tensor_copy(out=gain_rows[:], in_=gain_rows_bf16[:])
            gain_turned = bank([P, 2, 2, P], F32, "x")
            nc.tensor.transpose(gain_turned[:, 0, 0, :], gain_rows[:], identity[:])
            nc.vector.tensor_copy(out=gain_cols[:], in_=gain_turned[:, 0, 0, 0 : 2 * CHANNEL_TILES])

        def start_turned(half, c, on_vector):
            tokens = slice(half * HALF, (half + 1) * HALF)
            gain = gain_cols[:, c : c + 1]
            offset = gain_cols[:, CHANNEL_TILES + c : CHANNEL_TILES + c + 1]
            z_sums = bank([P, HALF], F32, "late z" if half == 1 else "z")
            nc.tensor.matmul_mx(
                out=z_sums[:],
                lhsT=u_words[:, c * P : (c + 1) * P].bitcast(FP8X4),
                lhsT_scale=u_scales[:, c * P : (c + 1) * P],
                rhs=h_words[:, tokens].bitcast(FP8X4),
                rhs_scale=h_scales[:, tokens],
                start=True,
                stop=True,
            )
            z_tile = pool.tile([P, HALF], F32, tag="z_tile", bufs=8)
            if on_vector:
                nc.vector.tensor_scalar(out=z_tile[:], in0=z_sums[:], scalar1=gain, scalar2=offset, op0=MULT, op1=ADD)
            else:
                nc.scalar.activation(out=z_tile[:], in_=z_sums[:], func=IDENTITY, scale=gain, bias=offset)
            return z_tile

        def turn_back(z_pair, a, first_col, result, role):
            z_back = bank([P, 2, PAIR], F32, role)
            for n in range(2):
                tokens = slice((2 * a + n) * P, (2 * a + n + 1) * P)
                for j in range(2):
                    nc.tensor.transpose(z_back[:, n, j * P : (j + 1) * P], z_pair[j][:, tokens], identity[:])
            nc.scalar.copy(out=result[:, :, first_col : first_col + PAIR], in_=z_back[:])

        def direct(half, chunk, tile, result):
            first = TURNED[half]
            width = U_CHUNK - first
            tokens = slice((half * TILES_PER_HALF + tile) * P, (half * TILES_PER_HALF + tile + 1) * P)
            z_gained = pool.tile([P, DIRECT], F32, tag="z_gained", bufs=4)
            for start in range(0, width, BANK):
                columns = min(BANK, width - start)
                u_cols = slice(chunk * U_CHUNK + first + start, chunk * U_CHUNK + first + start + columns)
                spread_cols = slice(first - min(TURNED) + start, first - min(TURNED) + start + columns)
                z_direct = bank([P, columns], F32, "late d" if half == 1 else "d")
                nc.tensor.matmul_mx(
                    out=z_direct[:],
                    lhsT=h_words[:, tokens].bitcast(FP8X4),
                    lhsT_scale=h_scales[:, tokens],
                    rhs=u_words[:, u_cols].bitcast(FP8X4),
                    rhs_scale=u_scales[:, u_cols],
                    start=True,
                    stop=True,
                )
                nc.vector.tensor_tensor(
                    out=z_gained[:, start : start + columns],
                    in0=z_direct[:],
                    in1=spread[:, chunk, 0, spread_cols],
                    op=MULT,
                )
            nc.gpsimd.tensor_tensor(
                out=result[:, tile % 2, first:U_CHUNK],
                in0=z_gained[:, 0:width],
                in1=spread[:, chunk, 1, first - min(TURNED) : DIRECT],
                op=ADD,
            )

        pieces = SLICES * STEPS
        GROUP_LAG = 5
        LAG = 4
        BACK_LAG = 4

        def spread_over_steps(step, count):
            return range(step * count // STEPS, (step + 1) * count // STEPS)

        def turn_u(n):
            chunk, b = divmod(n, STEPS)
            if b == 0:
                u_tiles[chunk] = pool.tile([P, U_CHUNK, PACK], BF16, tag="u_grouped", align_bytes=64, name="u_tile")
            turn_and_sign_u(u_raws[chunk], b, u_tiles[chunk], "first u" if chunk == 0 else "u")

        def turn_x(n):
            tile, b = divmod(n, STEPS)
            if b == 0:
                a_tiles[tile] = pool.tile([P, PASSES, P, PACK], BF16, tag="a_grouped", align_bytes=64, name="a_tile")
            turn_and_scale_x(
                x_raws[SLICES + tile][:, b * X_COLS : (b + 1) * X_COLS], 2 * b, a_tiles[tile][:, 2 * b : 2 * b + 2, :, :], "x"
            )

        def finish_piece(m, late):
            half, i = divmod(m, pieces)
            chunk, step = divmod(i, STEPS)
            units = TURNED[half] // PAIR
            for n in spread_over_steps(step, 2 * units):
                unit, a = divmod(n, 2)
                z_pair = (z_tiles[half, chunk, 2 * unit], z_tiles[half, chunk, 2 * unit + 1])
                turn_back(z_pair, a, unit * PAIR, results[half, chunk, a], "late back" if late else "back")
                if unit == units - 1:
                    first_tile = half * TILES_PER_HALF + 2 * a
                    nc.sync.dma_start(
                        out=out_view[:, first_tile : first_tile + 2, chunk * U_CHUNK : (chunk + 1) * U_CHUNK],
                        in_=results[half, chunk, a][:],
                    )

        def start_piece_z(m):
            half, i = divmod(m, pieces)
            chunk, step = divmod(i, STEPS)
            for t in spread_over_steps(step, TURNED[half] // P):
                z_tiles[half, chunk, t] = start_turned(half, chunk * (U_CHUNK // P) + t, half == 1 and t % 2 == 0)

        def start_piece_d(m):
            half, i = divmod(m, pieces)
            chunk, step = divmod(i, STEPS)
            if step % 2 == 0:
                results[half, chunk, step // 2] = big_tile([P, 2, U_CHUNK], F32)
            direct(half, chunk, step, results[half, chunk, step // 2])

        def multiply(group):
            tile, j = divmod(group, PACK)
            if j == 0:
                h_tiles[tile] = bank([P, PACK, P], F32, "h")
            first_matmul_group(j, second_packed[tile], h_tiles[tile])

        def quantising(k):
            group = k - GROUP_LAG
            if k % STEPS == STEPS - 1 and k < pieces:
                second_packed.append(pack_a(a_tiles[k // STEPS], PASSES, P))
            if k % STEPS == 0 and 0 < k < pieces:
                pack_u(k // STEPS, u_tiles[k // STEPS])
            if 0 < group <= pieces and group % PACK == 0:
                pack_tile(TILES_PER_HALF + group // PACK - 1, h_grouped[group // PACK - 1])
            if 0 <= group < pieces and group % PACK == PACK - 1:
                tile = group // PACK
                h_grouped[tile] = pool.tile([P, P, PACK], BF16, tag="h_grouped", align_bytes=64, name="h_tile")
                nc.scalar.copy(out=h_grouped[tile][:], in_=h_tiles[tile][:].rearrange("p j t -> p t j"))

        a_tiles = {}
        u_tiles = {}
        h_tiles = {}
        h_grouped = {}
        second_packed = []
        z_tiles = {}
        results = {}

        for n in range(STEPS):
            turn_u(n)
        for g in range(PASSES - V_PER_SLICE, PASSES):
            first_matmul_pass(g, a_packed, h_open)
        turn_gains()
        spread_first_rows()
        h_raw = pool.tile([P, PACK, HALF], BF16, tag="h_raw", bufs=1)
        h_first = pool.tile([P, HALF, PACK], BF16, tag="h_grouped", align_bytes=64)
        for j, h_bank in h_open:
            if j >= 2:
                nc.scalar.copy(out=h_raw[:, j, :], in_=h_bank[:])
            else:
                nc.vector.tensor_copy(out=h_raw[:, j, :], in_=h_bank[:])
        turn_x(0)
        pack_u(0, u_tiles[0])
        nc.vector.tensor_copy(out=h_first[:], in_=h_raw[:].rearrange("p j t -> p t j"))
        turn_x(1)
        nc.vector.quantize_mx(
            out=h_words[:, 0:HALF].bitcast(FP8X4),
            scales=h_scales[:, 0:HALF],
            in_=h_first[:].rearrange("p t j -> p (t j)"),
        )
        started = {}
        last_step = 22 + pieces + BACK_LAG
        k = 0
        while k < last_step:
            steps = range(k, min(k + (2 if k >= 16 else 1), last_step))
            k = steps.stop
            for n in steps:
                if LAG <= n < LAG + pieces:
                    started[n] = n - LAG
                elif 22 <= n < 22 + pieces:
                    started[n] = pieces + n - 22
                if STEPS + n < pieces:
                    turn_u(STEPS + n)
                if n - BACK_LAG in started:
                    finish_piece(started[n - BACK_LAG], n >= 22)
                if 1 < n < pieces:
                    turn_x(n)
            for n in steps:
                if n in started:
                    start_piece_d(started[n])
                if n in started:
                    start_piece_z(started[n])
                if 0 <= n - GROUP_LAG < pieces:
                    multiply(n - GROUP_LAG)
                quantising(n)
